import numpy as np
import ml_dtypes


def mxq(x, axis, fmt="e4m3"):
    dtype, down = {"e4m3": (ml_dtypes.float8_e4m3fn, 7), "e5m2": (ml_dtypes.float8_e5m2, 14)}[fmt]
    v = np.moveaxis(np.asarray(x, np.float32).astype(ml_dtypes.bfloat16).astype(np.float64), axis, -1)
    blocks = v.reshape(v.shape[:-1] + (-1, 32))
    amax = np.abs(blocks).max(-1, keepdims=True)
    byte = np.maximum(np.where(amax > 0, np.frexp(amax)[1] - 1 + 127, 0) - down, 1)
    scale = np.exp2(byte - 127.0)
    codes = (blocks / scale).astype(np.float32).astype(dtype).astype(np.float64)
    return np.moveaxis((codes * scale).reshape(v.shape), -1, axis)


WIDE = False


def mx_kscale(k):
    if not WIDE:
        return np.ones(k)
    levels = np.array([10, -10, 5, -5, 0])
    a = np.random.permutation(np.resize(levels, k // 512 * 4)).reshape(k // 512, 4)
    idx = np.arange(k)
    return np.exp2(a[idx // 512, idx % 128 // 32])


BF16 = ml_dtypes.bfloat16


def bf(x):
    return np.asarray(x, np.float32).astype(BF16)


def f64(x):
    return np.asarray(x).astype(np.float64)


N, X_DIM, Y_DIM, HID = 512, 8192, 512, 512


def setup_inputs():
    s = mx_kscale(X_DIM)
    t, u = mx_kscale(HID), mx_kscale(HID)
    col = 0.6 + 0.6 * np.random.standard_normal(Y_DIM)
    return {
        "x_samples": bf(np.random.standard_normal((N, X_DIM)) * s),
        "y_samples": bf(np.random.standard_normal((N, Y_DIM)) + col),
        "mu_W1": bf(np.random.standard_normal((X_DIM, HID)) / np.sqrt(X_DIM) / s[:, None] * t),
        "mu_b1": bf(np.random.standard_normal(HID) * 0.8 * t),
        "mu_W2": bf(np.random.standard_normal((HID, Y_DIM)) * 1.2 / np.sqrt(HID) / t[:, None]),
        "mu_b2": bf(0.4 + 0.4 * np.random.standard_normal(Y_DIM)),
        "lv_W1": bf(np.random.standard_normal((X_DIM, HID)) / np.sqrt(X_DIM) / s[:, None] * u),
        "lv_b1": bf(np.random.standard_normal(HID) * 0.8 * u),
        "lv_W2": bf(np.random.standard_normal((HID, Y_DIM)) / np.sqrt(HID) / u[:, None]),
        "lv_b2": bf(0.3 + 0.4 * np.random.standard_normal(Y_DIM)),
    }


def reference(x_samples, y_samples, mu_W1, mu_b1, mu_W2, mu_b2, lv_W1, lv_b1, lv_W2, lv_b2):
    x = f64(x_samples)
    y = f64(y_samples)
    xq = mxq(x, 1, "e4m3")
    h_mu = np.maximum((xq @ mxq(f64(mu_W1), 0, "e4m3")) + f64(mu_b1), 0.0)
    mu = (mxq(h_mu, 1, "e4m3") @ mxq(f64(mu_W2), 0, "e4m3")) + f64(mu_b2)
    h_lv = np.maximum((xq @ mxq(f64(lv_W1), 0, "e4m3")) + f64(lv_b1), 0.0)
    logvar = np.tanh((mxq(h_lv, 1, "e4m3") @ mxq(f64(lv_W2), 0, "e4m3")) + f64(lv_b2))
    w = 0.5 * np.exp(-logvar)
    n = x.shape[0]
    pos_row = -(((mu - y) ** 2) * w).sum(axis=1)
    Sy = y.sum(axis=0)
    Sy2 = (y ** 2).sum(axis=0)
    neg_row = -(w * (n * mu ** 2 - 2.0 * mu * Sy + Sy2)).sum(axis=1) / (n * n)
    return pos_row, neg_row

@@ -1,0 +1,302 @@
+from contextlib import ExitStack
+
+import concourse.mybir as mybir
+from concourse.masks import make_identity
+
+F32 = mybir.dt.float32
+BF16 = mybir.dt.bfloat16
+U32 = mybir.dt.uint32
+U8 = mybir.dt.uint8
+FP8X4 = mybir.dt.float8_e4m3fn_x4
+ACT = mybir.ActivationFunctionType
+ALU = mybir.AluOpType
+
+P = 128
+PACK = 4
+K_PASS = P * PACK
+
+N = 512
+X_DIM = 8192
+HID = 512
+Y_DIM = 512
+PASSES = X_DIM // K_PASS
+ROW_TILES = N // P
+D_TILES = Y_DIM // P
+BANKS = 8
+
+FLOPS = 2 * (2 * N * X_DIM * HID + 2 * N * HID * Y_DIM)
+
+X_LOADS = 2
+W1_PASSES_PER_LOAD = 2
+RUN = 4
+W1_VECTOR_COLUMNS = 256
+H_VECTOR_COLUMNS = 336
+
+MU_B1, LV_B1, MU_B2, LV_B2 = 0, 1, 2, 3
+
+
+def tile_infoncemi_pa_k_kernel(
+    tc, x_samples, y_samples, mu_W1, mu_b1, mu_W2, mu_b2, lv_W1, lv_b1, lv_W2, lv_b2, out_0, out_1
+):
+    nc = tc.nc
+    with ExitStack() as ctx:
+        const = ctx.enter_context(tc.tile_pool(name="const", bufs=1))
+        x_pool = ctx.enter_context(tc.tile_pool(name="x_pool", bufs=3))
+        xg_pool = ctx.enter_context(tc.tile_pool(name="xg_pool", bufs=4))
+        raw_pool = ctx.enter_context(tc.tile_pool(name="raw_pool", bufs=6))
+        grouped_pool = ctx.enter_context(tc.tile_pool(name="grouped_pool", bufs=4))
+        wq_pool = ctx.enter_context(tc.tile_pool(name="wq_pool", bufs=4))
+        h_pool = ctx.enter_context(tc.tile_pool(name="h_pool", bufs=1))
+        tail_pool = ctx.enter_context(tc.tile_pool(name="tail_pool", bufs=4))
+        psum = ctx.enter_context(tc.psum_pool(name="psum", bufs=1))
+
+        def bank(index, shape, dtype, name):
+            return psum.tile(shape, dtype, name=name, tag="bank%d" % index)
+
+        def regroup(dst, src, vector_columns):
+            dst_runs = dst.rearrange("p (c i) t -> p c t i", i=RUN)
+            src_runs = src.rearrange("p t (c i) -> p c t i", i=RUN)
+            split = vector_columns // RUN
+            nc.vector.tensor_copy(out=dst_runs[:, :split], in_=src_runs[:, :split])
+            nc.scalar.copy(out=dst_runs[:, split:], in_=src_runs[:, split:])
+
+        def quantise(grouped, codes, scales):
+            nc.vector.quantize_mx(
+                out=codes.bitcast(FP8X4), scales=scales, in_=grouped.rearrange("p c t -> p (c t)")
+            )
+
+        ident_f32 = const.tile([P, P], F32)
+        make_identity(nc, ident_f32[:])
+        ident_bf16 = const.tile([P, P], BF16)
+        make_identity(nc, ident_bf16[:])
+        pos_weight = const.tile([P, P], F32)
+        nc.vector.memset(pos_weight[:], -0.5)
+        neg_weight = const.tile([P, P], F32)
+        nc.vector.memset(neg_weight[:], -0.5 / N)
+
+        bias_rows = const.tile([P, P], BF16)
+        nc.vector.memset(bias_rows[:], 0.0)
+        for place, vector in enumerate((mu_b1, lv_b1, mu_b2, lv_b2)):
+            nc.scalar.dma_start(
+                out=bias_rows[PACK * place : PACK * (place + 1), :],
+                in_=vector.rearrange("(m p) -> m p", p=P),
+            )
+        y_rows = const.tile([P, ROW_TILES, Y_DIM], BF16)
+        nc.sync.dma_start(out=y_rows[:], in_=y_samples.rearrange("(r p) d -> p r d", p=P))
+        w2_raw = {}
+        for head, w2 in (("mu", mu_W2), ("lv", lv_W2)):
+            w2_raw[head] = raw_pool.tile([P, PACK, Y_DIM], BF16, name="w2_raw", tag="raw")
+            nc.sync.dma_start(out=w2_raw[head][:], in_=w2.rearrange("(t p) d -> p t d", p=P))
+
+        bias_ps = bank(4, [P, P], BF16, "bias_ps")
+        nc.tensor.transpose(bias_ps[:], bias_rows[:], ident_bf16[:])
+        bias_cols = const.tile([P, 4 * PACK], F32)
+        nc.vector.tensor_copy(out=bias_cols[:], in_=bias_ps[:, 0 : 4 * PACK])
+
+        def bias_column(place, m):
+            return bias_cols[:, PACK * place + m : PACK * place + m + 1]
+
+        y_t = const.tile([P, D_TILES, N], BF16)
+        y_squares = const.tile([P, D_TILES, N], BF16)
+        sum_y = const.tile([P, D_TILES], F32)
+        sum_y2 = const.tile([P, D_TILES], F32)
+        for j in range(D_TILES):
+            yt_ps = bank(j, [P, N], BF16, "yt_ps")
+            for r in range(ROW_TILES):
+                nc.tensor.transpose(
+                    yt_ps[:, r * P : (r + 1) * P], y_rows[:, r, j * P : (j + 1) * P], ident_bf16[:]
+                )
+            nc.scalar.activation(
+                out=y_t[:, j, :], in_=yt_ps[:], func=ACT.Copy, accum_out=sum_y[:, j : j + 1]
+            )
+            nc.scalar.activation(
+                out=y_squares[:, j, :], in_=yt_ps[:], func=ACT.Square, accum_out=sum_y2[:, j : j + 1]
+            )
+        mean_y = const.tile([P, D_TILES], F32)
+        nc.vector.tensor_scalar(
+            out=mean_y[:], in0=sum_y[:], scalar1=1.0 / N, scalar2=None, op0=ALU.mult
+        )
+        mean_sq = const.tile([P, D_TILES], F32)
+        nc.vector.tensor_tensor(out=mean_sq[:], in0=mean_y[:], in1=mean_y[:], op=ALU.mult)
+        var_y = const.tile([P, D_TILES], F32)
+        nc.vector.scalar_tensor_tensor(
+            out=var_y[:], in0=sum_y2[:], scalar=1.0 / N, in1=mean_sq[:], op0=ALU.mult, op1=ALU.subtract
+        )
+        centre = const.tile([P, D_TILES], F32)
+        nc.vector.tensor_tensor(
+            out=centre[:],
+            in0=bias_cols[:, PACK * MU_B2 : PACK * (MU_B2 + 1)],
+            in1=mean_y[:],
+            op=ALU.subtract,
+        )
+
+        w2_codes = {}
+        w2_scales = {}
+        for head in ("mu", "lv"):
+            w2_grouped = grouped_pool.tile([P, Y_DIM, PACK], BF16, align_bytes=64, tag="grouped")
+            regroup(w2_grouped[:], w2_raw[head][:], W1_VECTOR_COLUMNS)
+            w2_codes[head] = const.tile([P, Y_DIM], U32, align_bytes=64, name="w2_codes_" + head)
+            w2_scales[head] = const.tile([P, Y_DIM], U8, align_bytes=64, name="w2_scales_" + head)
+            quantise(w2_grouped[:], w2_codes[head][:], w2_scales[head][:])
+
+        x_codes = const.tile([P, PASSES, N], U32, align_bytes=64)
+        x_scales = const.tile([P, PASSES, N], U8, align_bytes=64)
+        for r in range(ROW_TILES):
+            x_rows = x_pool.tile([P, X_DIM], BF16)
+            for part in range(X_LOADS):
+                cols = slice(part * X_DIM // X_LOADS, (part + 1) * X_DIM // X_LOADS)
+                nc.sync.dma_start(out=x_rows[:, cols], in_=x_samples[r * P : (r + 1) * P, cols])
+            x_words = x_rows[:].bitcast(F32)
+            for pair in range(PASSES // 2):
+                xt_ps = bank(pair % BANKS, [P, 2, 2, P], F32, "xt_ps")
+                for g2 in range(2):
+                    for u in range(2):
+                        first = (2 * pair + g2) * (K_PASS // 2) + u * P
+                        nc.tensor.transpose(
+                            xt_ps[:, g2, u, :], x_words[:, first : first + P], ident_f32[:]
+                        )
+                x_grouped = xg_pool.tile([P, 2, P * PACK], BF16, align_bytes=64)
+                word_view = x_grouped[:].rearrange("p g c -> p (g c)").bitcast(F32)
+                copy_out = word_view.rearrange("p (g n u) -> p g n u", g=2, u=2)
+                copy_in = xt_ps[:].rearrange("p g u n -> p g n u")
+                if pair % 4 == 3:
+                    nc.vector.tensor_copy(out=copy_out, in_=copy_in)
+                else:
+                    nc.scalar.copy(out=copy_out, in_=copy_in)
+                for g2 in range(2):
+                    g = 2 * pair + g2
+                    nc.vector.quantize_mx(
+                        out=x_codes[:, g, r * P : (r + 1) * P].bitcast(FP8X4),
+                        scales=x_scales[:, g, r * P : (r + 1) * P],
+                        in_=x_grouped[:, g2, :],
+                    )
+
+        def first_layer(w1, acc):
+            def quantise_and_multiply(g, grouped):
+                w_codes = wq_pool.tile([P, HID], U32, align_bytes=64)
+                w_scales = wq_pool.tile([P, HID], U8, align_bytes=64)
+                quantise(grouped[:], w_codes[:], w_scales[:])
+                for m in range(PACK):
+                    nc.tensor.matmul_mx(
+                        out=acc[m][:],
+                        lhsT=w_codes[:, m * P : (m + 1) * P].bitcast(FP8X4),
+                        lhsT_scale=w_scales[:, m * P : (m + 1) * P],
+                        rhs=x_codes[:, g, :].bitcast(FP8X4),
+                        rhs_scale=x_scales[:, g, :],
+                        start=(g == 0),
+                        stop=(g == PASSES - 1),
+                    )
+
+            waiting = None
+            for load in range(PASSES // W1_PASSES_PER_LOAD):
+                rows = slice(
+                    load * W1_PASSES_PER_LOAD * K_PASS, (load + 1) * W1_PASSES_PER_LOAD * K_PASS
+                )
+                raw = raw_pool.tile([P, W1_PASSES_PER_LOAD, PACK, HID], BF16, tag="raw")
+                nc.sync.dma_start(
+                    out=raw[:].rearrange("p g (u e) h -> p (g u) e h", e=2),
+                    in_=w1[rows, :].rearrange("(s p e) h -> p s e h", p=P, e=2),
+                )
+                for g2 in range(W1_PASSES_PER_LOAD):
+                    grouped = grouped_pool.tile([P, HID, PACK], BF16, align_bytes=64, tag="grouped")
+                    regroup(grouped[:], raw[:, g2], W1_VECTOR_COLUMNS)
+                    if waiting is not None:
+                        quantise_and_multiply(waiting[0], waiting[1])
+                    waiting = (load * W1_PASSES_PER_LOAD + g2, grouped)
+            quantise_and_multiply(waiting[0], waiting[1])
+
+        def second_layer(head, acc, b1_place, first_bank):
+            h_rows = h_pool.tile([P, PACK, N], BF16)
+            for m in range(PACK):
+                if m % 2 == 0:
+                    nc.scalar.activation(
+                        out=h_rows[:, m, :], in_=acc[m][:], func=ACT.Relu, bias=bias_column(b1_place, m)
+                    )
+                else:
+                    nc.vector.tensor_scalar(
+                        out=h_rows[:, m, :],
+                        in0=acc[m][:],
+                        scalar1=bias_column(b1_place, m),
+                        scalar2=0.0,
+                        op0=ALU.add,
+                        op1=ALU.max,
+                    )
+            h_grouped = grouped_pool.tile([P, N, PACK], BF16, align_bytes=64, tag="grouped")
+            regroup(h_grouped[:], h_rows[:], H_VECTOR_COLUMNS)
+            h_codes = h_pool.tile([P, N], U32, align_bytes=64)
+            h_scales = h_pool.tile([P, N], U8, align_bytes=64)
+            quantise(h_grouped[:], h_codes[:], h_scales[:])
+            products = []
+            for j in range(D_TILES):
+                product = bank(first_bank + j, [P, N], F32, "product")
+                nc.tensor.matmul_mx(
+                    out=product[:],
+                    lhsT=w2_codes[head][:, j * P : (j + 1) * P].bitcast(FP8X4),
+                    lhsT_scale=w2_scales[head][:, j * P : (j + 1) * P],
+                    rhs=h_codes[:].bitcast(FP8X4),
+                    rhs_scale=h_scales[:],
+                    start=True,
+                    stop=True,
+                )
+                products.append(product)
+            return products
+
+        mu_acc = [bank(m, [P, N], F32, "mu_acc") for m in range(PACK)]
+        first_layer(mu_W1, mu_acc)
+        mu_t = second_layer("mu", mu_acc, MU_B1, 0)
+        pos_terms = []
+        neg_terms = []
+        for j in range(D_TILES):
+            pos_term = const.tile([P, N], F32, name="pos_term%d" % j)
+            nc.vector.scalar_tensor_tensor(
+                out=pos_term[:],
+                in0=mu_t[j][:],
+                scalar=bias_column(MU_B2, j),
+                in1=y_t[:, j, :],
+                op0=ALU.add,
+                op1=ALU.subtract,
+            )
+            nc.scalar.activation(out=pos_term[:], in_=pos_term[:], func=ACT.Square)
+            neg_term = const.tile([P, N], F32, name="neg_term%d" % j)
+            nc.scalar.activation(
+                out=neg_term[:], in_=mu_t[j][:], func=ACT.Square, bias=centre[:, j : j + 1]
+            )
+            pos_terms.append(pos_term)
+            neg_terms.append(neg_term)
+
+        lv_acc = [bank(PACK + m, [P, N], F32, "lv_acc") for m in range(PACK)]
+        first_layer(lv_W1, lv_acc)
+        lv_t = second_layer("lv", lv_acc, LV_B1, PACK)
+
+        pos_sum = bank(0, [P, N], F32, "pos_sum")
+        neg_sum = bank(1, [P, N], F32, "neg_sum")
+        for j in range(D_TILES):
+            weight = tail_pool.tile([P, N], F32)
+            nc.scalar.activation(
+                out=weight[:], in_=lv_t[j][:], func=ACT.Tanh, bias=bias_column(LV_B2, j)
+            )
+            nc.scalar.activation(out=weight[:], in_=weight[:], func=ACT.Exp, scale=-1.0)
+            nc.vector.tensor_tensor(
+                out=pos_terms[j][:], in0=pos_terms[j][:], in1=weight[:], op=ALU.mult
+            )
+            nc.vector.scalar_tensor_tensor(
+                out=neg_terms[j][:],
+                in0=neg_terms[j][:],
+                scalar=var_y[:, j : j + 1],
+                in1=weight[:],
+                op0=ALU.add,
+                op1=ALU.mult,
+            )
+            nc.tensor.matmul(
+                out=pos_sum[:], lhsT=pos_weight[:], rhs=pos_terms[j][:],
+                start=(j == 0), stop=(j == D_TILES - 1),
+            )
+            nc.tensor.matmul(
+                out=neg_sum[:], lhsT=neg_weight[:], rhs=neg_terms[j][:],
+                start=(j == 0), stop=(j == D_TILES - 1),
+            )
+        result = const.tile([P, 2, N], F32)
+        nc.scalar.copy(out=result[:, 0, :], in_=pos_sum[:])
+        nc.vector.tensor_copy(out=result[:, 1, :], in_=neg_sum[:])
+        nc.sync.dma_start(out=out_0.rearrange("(o n) -> o n", o=1), in_=result[0:1, 0, :])
+        nc.sync.dma_start(out=out_1.rearrange("(o n) -> o n", o=1), in_=result[0:1, 1, :])

@@ -26,11 +26,14 @@ BANKS = 8
 
 FLOPS = 2 * (2 * N * X_DIM * HID + 2 * N * HID * Y_DIM)
 
-X_LOADS = 2
+X_PIECES = 2
+PIECE_PASSES = PASSES // X_PIECES
 W1_PASSES_PER_LOAD = 2
+RAW_BUFS = 6
 RUN = 4
 W1_VECTOR_COLUMNS = 256
 H_VECTOR_COLUMNS = 336
+EPILOGUE_LAG = 2
 
 MU_B1, LV_B1, MU_B2, LV_B2 = 0, 1, 2, 3
 
@@ -41,28 +44,22 @@ def tile_infoncemi_pa_k_kernel(
     nc = tc.nc
     with ExitStack() as ctx:
         const = ctx.enter_context(tc.tile_pool(name="const", bufs=1))
-        x_pool = ctx.enter_context(tc.tile_pool(name="x_pool", bufs=3))
-        xg_pool = ctx.enter_context(tc.tile_pool(name="xg_pool", bufs=4))
-        raw_pool = ctx.enter_context(tc.tile_pool(name="raw_pool", bufs=6))
-        grouped_pool = ctx.enter_context(tc.tile_pool(name="grouped_pool", bufs=4))
-        wq_pool = ctx.enter_context(tc.tile_pool(name="wq_pool", bufs=4))
-        h_pool = ctx.enter_context(tc.tile_pool(name="h_pool", bufs=1))
-        tail_pool = ctx.enter_context(tc.tile_pool(name="tail_pool", bufs=4))
+        raw_pool = ctx.enter_context(tc.tile_pool(name="raw_pool", bufs=RAW_BUFS))
         psum = ctx.enter_context(tc.psum_pool(name="psum", bufs=1))
 
         def bank(index, shape, dtype, name):
-            return psum.tile(shape, dtype, name=name, tag="bank%d" % index)
+            return psum.tile(shape, dtype, name=name, tag="bank%d" % (index % BANKS))
 
         def regroup(dst, src, vector_columns):
-            dst_runs = dst.rearrange("p (c i) t -> p c t i", i=RUN)
-            src_runs = src.rearrange("p t (c i) -> p c t i", i=RUN)
+            dst_runs = dst.rearrange("p g (c i) t -> p g c t i", i=RUN)
+            src_runs = src.rearrange("p g t (c i) -> p g c t i", i=RUN)
             split = vector_columns // RUN
-            nc.vector.tensor_copy(out=dst_runs[:, :split], in_=src_runs[:, :split])
-            nc.scalar.copy(out=dst_runs[:, split:], in_=src_runs[:, split:])
+            nc.vector.tensor_copy(out=dst_runs[:, :, :split], in_=src_runs[:, :, :split])
+            nc.scalar.copy(out=dst_runs[:, :, split:], in_=src_runs[:, :, split:])
 
         def quantise(grouped, codes, scales):
             nc.vector.quantize_mx(
-                out=codes.bitcast(FP8X4), scales=scales, in_=grouped.rearrange("p c t -> p (c t)")
+                out=codes.bitcast(FP8X4), scales=scales, in_=grouped.rearrange("p g c t -> p (g c t)")
             )
 
         ident_f32 = const.tile([P, P], F32)
@@ -73,160 +70,224 @@ def tile_infoncemi_pa_k_kernel(
         nc.vector.memset(pos_weight[:], -0.5)
         neg_weight = const.tile([P, P], F32)
         nc.vector.memset(neg_weight[:], -0.5 / N)
-
         bias_rows = const.tile([P, P], BF16)
         nc.vector.memset(bias_rows[:], 0.0)
-        for place, vector in enumerate((mu_b1, lv_b1, mu_b2, lv_b2)):
-            nc.scalar.dma_start(
-                out=bias_rows[PACK * place : PACK * (place + 1), :],
-                in_=vector.rearrange("(m p) -> m p", p=P),
-            )
-        y_rows = const.tile([P, ROW_TILES, Y_DIM], BF16)
-        nc.sync.dma_start(out=y_rows[:], in_=y_samples.rearrange("(r p) d -> p r d", p=P))
-        w2_raw = {}
-        for head, w2 in (("mu", mu_W2), ("lv", lv_W2)):
-            w2_raw[head] = raw_pool.tile([P, PACK, Y_DIM], BF16, name="w2_raw", tag="raw")
-            nc.sync.dma_start(out=w2_raw[head][:], in_=w2.rearrange("(t p) d -> p t d", p=P))
 
-        bias_ps = bank(4, [P, P], BF16, "bias_ps")
-        nc.tensor.transpose(bias_ps[:], bias_rows[:], ident_bf16[:])
+        x_codes = const.tile([P, PASSES, N], U32, align_bytes=64)
+        x_scales = const.tile([P, PASSES, N], U8, align_bytes=64)
+        y_t = const.tile([P, D_TILES, N], BF16)
         bias_cols = const.tile([P, 4 * PACK], F32)
-        nc.vector.tensor_copy(out=bias_cols[:], in_=bias_ps[:, 0 : 4 * PACK])
+        var_y = const.tile([P, D_TILES], F32)
+        centre = const.tile([P, D_TILES], F32)
+        w2_codes = {}
+        w2_scales = {}
+        for head in ("mu", "lv"):
+            w2_codes[head] = const.tile([P, Y_DIM], U32, align_bytes=64, name="w2_codes_" + head)
+            w2_scales[head] = const.tile([P, Y_DIM], U8, align_bytes=64, name="w2_scales_" + head)
 
         def bias_column(place, m):
             return bias_cols[:, PACK * place + m : PACK * place + m + 1]
 
-        y_t = const.tile([P, D_TILES, N], BF16)
-        y_squares = const.tile([P, D_TILES, N], BF16)
-        sum_y = const.tile([P, D_TILES], F32)
-        sum_y2 = const.tile([P, D_TILES], F32)
-        for j in range(D_TILES):
-            yt_ps = bank(j, [P, N], BF16, "yt_ps")
-            for r in range(ROW_TILES):
-                nc.tensor.transpose(
-                    yt_ps[:, r * P : (r + 1) * P], y_rows[:, r, j * P : (j + 1) * P], ident_bf16[:]
-                )
-            nc.scalar.activation(
-                out=y_t[:, j, :], in_=yt_ps[:], func=ACT.Copy, accum_out=sum_y[:, j : j + 1]
-            )
-            nc.scalar.activation(
-                out=y_squares[:, j, :], in_=yt_ps[:], func=ACT.Square, accum_out=sum_y2[:, j : j + 1]
-            )
-        mean_y = const.tile([P, D_TILES], F32)
-        nc.vector.tensor_scalar(
-            out=mean_y[:], in0=sum_y[:], scalar1=1.0 / N, scalar2=None, op0=ALU.mult
-        )
-        mean_sq = const.tile([P, D_TILES], F32)
-        nc.vector.tensor_tensor(out=mean_sq[:], in0=mean_y[:], in1=mean_y[:], op=ALU.mult)
-        var_y = const.tile([P, D_TILES], F32)
-        nc.vector.scalar_tensor_tensor(
-            out=var_y[:], in0=sum_y2[:], scalar=1.0 / N, in1=mean_sq[:], op0=ALU.mult, op1=ALU.subtract
-        )
-        centre = const.tile([P, D_TILES], F32)
-        nc.vector.tensor_tensor(
-            out=centre[:],
-            in0=bias_cols[:, PACK * MU_B2 : PACK * (MU_B2 + 1)],
-            in1=mean_y[:],
-            op=ALU.subtract,
-        )
-
-        w2_codes = {}
-        w2_scales = {}
-        for head in ("mu", "lv"):
-            w2_grouped = grouped_pool.tile([P, Y_DIM, PACK], BF16, align_bytes=64, tag="grouped")
-            regroup(w2_grouped[:], w2_raw[head][:], W1_VECTOR_COLUMNS)
-            w2_codes[head] = const.tile([P, Y_DIM], U32, align_bytes=64, name="w2_codes_" + head)
-            w2_scales[head] = const.tile([P, Y_DIM], U8, align_bytes=64, name="w2_scales_" + head)
-            quantise(w2_grouped[:], w2_codes[head][:], w2_scales[head][:])
-
-        x_codes = const.tile([P, PASSES, N], U32, align_bytes=64)
-        x_scales = const.tile([P, PASSES, N], U8, align_bytes=64)
-        for r in range(ROW_TILES):
-            x_rows = x_pool.tile([P, X_DIM], BF16)
-            for part in range(X_LOADS):
-                cols = slice(part * X_DIM // X_LOADS, (part + 1) * X_DIM // X_LOADS)
-                nc.sync.dma_start(out=x_rows[:, cols], in_=x_samples[r * P : (r + 1) * P, cols])
-            x_words = x_rows[:].bitcast(F32)
-            for pair in range(PASSES // 2):
-                xt_ps = bank(pair % BANKS, [P, 2, 2, P], F32, "xt_ps")
-                for g2 in range(2):
-                    for u in range(2):
-                        first = (2 * pair + g2) * (K_PASS // 2) + u * P
-                        nc.tensor.transpose(
-                            xt_ps[:, g2, u, :], x_words[:, first : first + P], ident_f32[:]
-                        )
-                x_grouped = xg_pool.tile([P, 2, P * PACK], BF16, align_bytes=64)
-                word_view = x_grouped[:].rearrange("p g c -> p (g c)").bitcast(F32)
-                copy_out = word_view.rearrange("p (g n u) -> p g n u", g=2, u=2)
-                copy_in = xt_ps[:].rearrange("p g u n -> p g n u")
-                if pair % 4 == 3:
-                    nc.vector.tensor_copy(out=copy_out, in_=copy_in)
+        loads = []
+        for head, w1 in (("mu", mu_W1), ("lv", lv_W1)):
+            for first in range(0, PASSES, W1_PASSES_PER_LOAD):
+                if head == "lv" and first == PASSES - W1_PASSES_PER_LOAD:
+                    for g in range(first, PASSES):
+                        loads.append((head, w1, g, 1))
                 else:
-                    nc.scalar.copy(out=copy_out, in_=copy_in)
-                for g2 in range(2):
-                    g = 2 * pair + g2
-                    nc.vector.quantize_mx(
-                        out=x_codes[:, g, r * P : (r + 1) * P].bitcast(FP8X4),
-                        scales=x_scales[:, g, r * P : (r + 1) * P],
-                        in_=x_grouped[:, g2, :],
-                    )
+                    loads.append((head, w1, first, W1_PASSES_PER_LOAD))
+        raw_tiles = {}
 
-        def first_layer(w1, acc):
-            def quantise_and_multiply(g, grouped):
-                w_codes = wq_pool.tile([P, HID], U32, align_bytes=64)
-                w_scales = wq_pool.tile([P, HID], U8, align_bytes=64)
-                quantise(grouped[:], w_codes[:], w_scales[:])
+        def start_load(k):
+            if k >= len(loads):
+                return
+            head, w1, first, passes = loads[k]
+            raw = raw_pool.tile([P, passes, PACK, HID], BF16, name="raw", tag="raw")
+            nc.sync.dma_start(
+                out=raw[:].rearrange("p g (u e) h -> p (g u) e h", e=2),
+                in_=w1[first * K_PASS : (first + passes) * K_PASS, :].rearrange(
+                    "(s p e) h -> p s e h", p=P, e=2
+                ),
+            )
+            raw_tiles[k] = raw
+
+        with ExitStack() as phase1:
+            x_pool = phase1.enter_context(tc.tile_pool(name="x_pool", bufs=ROW_TILES * X_PIECES))
+            xg_pool = phase1.enter_context(tc.tile_pool(name="xg_pool", bufs=4))
+            prep = phase1.enter_context(tc.tile_pool(name="prep", bufs=1))
+
+            for place, vector in enumerate((mu_b1, lv_b1, mu_b2, lv_b2)):
+                nc.scalar.dma_start(
+                    out=bias_rows[PACK * place : PACK * (place + 1), :],
+                    in_=vector.rearrange("(m p) -> m p", p=P),
+                )
+            x_rows = {}
+
+            def load_x(r):
+                for piece in range(X_PIECES):
+                    x_rows[r, piece] = x_pool.tile([P, X_DIM // X_PIECES], BF16, name="x_rows", tag="x_rows")
+                    cols = slice(piece * X_DIM // X_PIECES, (piece + 1) * X_DIM // X_PIECES)
+                    nc.sync.dma_start(out=x_rows[r, piece][:], in_=x_samples[r * P : (r + 1) * P, cols])
+
+            w2_raw = {}
+
+            def load_w2(head, w2):
+                w2_raw[head] = prep.tile([P, 1, PACK, Y_DIM], BF16, name="w2_raw_" + head)
+                nc.sync.dma_start(
+                    out=w2_raw[head][:, 0], in_=w2.rearrange("(t p) d -> p t d", p=P)
+                )
+
+            y_rows = prep.tile([P, ROW_TILES, Y_DIM], BF16)
+            load_x(0)
+            nc.sync.dma_start(out=y_rows[:], in_=y_samples.rearrange("(r p) d -> p r d", p=P))
+            load_x(1)
+            load_w2("mu", mu_W2)
+            load_x(2)
+            load_w2("lv", lv_W2)
+            load_x(3)
+            for k in range(RAW_BUFS):
+                start_load(k)
+
+            def x_to_mx(r):
+                for piece in range(X_PIECES):
+                    x_words = x_rows[r, piece][:].bitcast(F32)
+                    for pair in range(PIECE_PASSES // 2):
+                        xt_ps = bank(piece * (PIECE_PASSES // 2) + pair, [P, 2, 2, P], F32, "xt_ps")
+                        for g2 in range(2):
+                            for u in range(2):
+                                first = (2 * pair + g2) * (K_PASS // 2) + u * P
+                                nc.tensor.transpose(
+                                    xt_ps[:, g2, u, :], x_words[:, first : first + P], ident_f32[:]
+                                )
+                        x_grouped = xg_pool.tile([P, 2, P * PACK], BF16, align_bytes=64)
+                        word_view = x_grouped[:].rearrange("p g c -> p (g c)").bitcast(F32)
+                        copy_out = word_view.rearrange("p (g n u) -> p g n u", g=2, u=2)
+                        copy_in = xt_ps[:].rearrange("p g u n -> p g n u")
+                        if pair % 4 == 3:
+                            nc.vector.tensor_copy(out=copy_out, in_=copy_in)
+                        else:
+                            nc.scalar.copy(out=copy_out, in_=copy_in)
+                        for g2 in range(2):
+                            g = piece * PIECE_PASSES + 2 * pair + g2
+                            nc.vector.quantize_mx(
+                                out=x_codes[:, g, r * P : (r + 1) * P].bitcast(FP8X4),
+                                scales=x_scales[:, g, r * P : (r + 1) * P],
+                                in_=x_grouped[:, g2, :],
+                            )
+
+            def y_and_biases():
+                bias_ps = bank(4, [P, P], BF16, "bias_ps")
+                nc.tensor.transpose(bias_ps[:], bias_rows[:], ident_bf16[:])
+                nc.vector.tensor_copy(out=bias_cols[:], in_=bias_ps[:, 0 : 4 * PACK])
+                y_squares = prep.tile([P, D_TILES, N], BF16)
+                sum_y = prep.tile([P, D_TILES], F32)
+                sum_y2 = prep.tile([P, D_TILES], F32)
+                for j in range(D_TILES):
+                    yt_ps = bank(j, [P, N], BF16, "yt_ps")
+                    for r in range(ROW_TILES):
+                        nc.tensor.transpose(
+                            yt_ps[:, r * P : (r + 1) * P], y_rows[:, r, j * P : (j + 1) * P], ident_bf16[:]
+                        )
+                    nc.scalar.activation(
+                        out=y_t[:, j, :], in_=yt_ps[:], func=ACT.Copy, accum_out=sum_y[:, j : j + 1]
+                    )
+                    nc.scalar.activation(
+                        out=y_squares[:, j, :], in_=y_t[:, j, :], func=ACT.Square,
+                        accum_out=sum_y2[:, j : j + 1],
+                    )
+                mean_y = prep.tile([P, D_TILES], F32)
+                nc.vector.tensor_scalar(
+                    out=mean_y[:], in0=sum_y[:], scalar1=1.0 / N, scalar2=None, op0=ALU.mult
+                )
+                mean_sq = prep.tile([P, D_TILES], F32)
+                nc.vector.tensor_tensor(out=mean_sq[:], in0=mean_y[:], in1=mean_y[:], op=ALU.mult)
+                nc.vector.scalar_tensor_tensor(
+                    out=var_y[:], in0=sum_y2[:], scalar=1.0 / N, in1=mean_sq[:],
+                    op0=ALU.mult, op1=ALU.subtract,
+                )
+                nc.vector.tensor_tensor(
+                    out=centre[:], in0=bias_cols[:, PACK * MU_B2 : PACK * (MU_B2 + 1)], in1=mean_y[:],
+                    op=ALU.subtract,
+                )
+
+            def w2_to_mx(head):
+                w2_grouped = prep.tile([P, 1, Y_DIM, PACK], BF16, align_bytes=64, name="w2_grouped_" + head)
+                regroup(w2_grouped[:], w2_raw[head][:], W1_VECTOR_COLUMNS)
+                quantise(w2_grouped[:], w2_codes[head][:], w2_scales[head][:])
+
+            x_to_mx(0)
+            y_and_biases()
+            x_to_mx(1)
+            w2_to_mx("mu")
+            x_to_mx(2)
+            w2_to_mx("lv")
+            x_to_mx(3)
+
+        grouped_pool = ctx.enter_context(tc.tile_pool(name="grouped_pool", bufs=3, reuse_waits="tile"))
+        wq_pool = ctx.enter_context(tc.tile_pool(name="wq_pool", bufs=3, reuse_waits="tile"))
+        h_pool = ctx.enter_context(tc.tile_pool(name="h_pool", bufs=1, reuse_waits="tile"))
+        term_pool = ctx.enter_context(tc.tile_pool(name="term_pool", bufs=1, reuse_waits="tile"))
+        tail_pool = ctx.enter_context(tc.tile_pool(name="tail_pool", bufs=3, reuse_waits="tile"))
+
+        acc = {
+            "mu": [bank(m, [P, N], F32, "mu_acc") for m in range(PACK)],
+            "lv": [bank(PACK + m, [P, N], F32, "lv_acc") for m in range(PACK)],
+        }
+        grouped_tiles = {}
+
+        def regroup_load(k):
+            passes = loads[k][3]
+            grouped_tiles[k] = grouped_pool.tile(
+                [P, passes, HID, PACK], BF16, align_bytes=64, name="grouped", tag="grouped"
+            )
+            regroup(grouped_tiles[k][:], raw_tiles[k][:], W1_VECTOR_COLUMNS)
+
+        def quantise_and_multiply(k):
+            head, w1, first, passes = loads[k]
+            w_codes = wq_pool.tile([P, passes * HID], U32, align_bytes=64, name="w_codes", tag="w_codes")
+            w_scales = wq_pool.tile([P, passes * HID], U8, align_bytes=64, name="w_scales", tag="w_scales")
+            quantise(grouped_tiles[k][:], w_codes[:], w_scales[:])
+            for g2 in range(passes):
+                g = first + g2
                 for m in range(PACK):
+                    cols = slice(g2 * HID + m * P, g2 * HID + (m + 1) * P)
                     nc.tensor.matmul_mx(
-                        out=acc[m][:],
-                        lhsT=w_codes[:, m * P : (m + 1) * P].bitcast(FP8X4),
-                        lhsT_scale=w_scales[:, m * P : (m + 1) * P],
+                        out=acc[head][m][:],
+                        lhsT=w_codes[:, cols].bitcast(FP8X4),
+                        lhsT_scale=w_scales[:, cols],
                         rhs=x_codes[:, g, :].bitcast(FP8X4),
                         rhs_scale=x_scales[:, g, :],
                         start=(g == 0),
                         stop=(g == PASSES - 1),
                     )
 
-            waiting = None
-            for load in range(PASSES // W1_PASSES_PER_LOAD):
-                rows = slice(
-                    load * W1_PASSES_PER_LOAD * K_PASS, (load + 1) * W1_PASSES_PER_LOAD * K_PASS
-                )
-                raw = raw_pool.tile([P, W1_PASSES_PER_LOAD, PACK, HID], BF16, tag="raw")
-                nc.sync.dma_start(
-                    out=raw[:].rearrange("p g (u e) h -> p (g u) e h", e=2),
-                    in_=w1[rows, :].rearrange("(s p e) h -> p s e h", p=P, e=2),
-                )
-                for g2 in range(W1_PASSES_PER_LOAD):
-                    grouped = grouped_pool.tile([P, HID, PACK], BF16, align_bytes=64, tag="grouped")
-                    regroup(grouped[:], raw[:, g2], W1_VECTOR_COLUMNS)
-                    if waiting is not None:
-                        quantise_and_multiply(waiting[0], waiting[1])
-                    waiting = (load * W1_PASSES_PER_LOAD + g2, grouped)
-            quantise_and_multiply(waiting[0], waiting[1])
+        h_grouped = {}
 
-        def second_layer(head, acc, b1_place, first_bank):
-            h_rows = h_pool.tile([P, PACK, N], BF16)
+        def hidden(head, b1_place):
+            h_rows = h_pool.tile([P, 1, PACK, N], BF16, name="h_rows", tag="h_rows")
             for m in range(PACK):
                 if m % 2 == 0:
                     nc.scalar.activation(
-                        out=h_rows[:, m, :], in_=acc[m][:], func=ACT.Relu, bias=bias_column(b1_place, m)
+                        out=h_rows[:, 0, m, :], in_=acc[head][m][:], func=ACT.Relu,
+                        bias=bias_column(b1_place, m),
                     )
                 else:
                     nc.vector.tensor_scalar(
-                        out=h_rows[:, m, :],
-                        in0=acc[m][:],
-                        scalar1=bias_column(b1_place, m),
-                        scalar2=0.0,
-                        op0=ALU.add,
-                        op1=ALU.max,
+                        out=h_rows[:, 0, m, :], in0=acc[head][m][:], scalar1=bias_column(b1_place, m),
+                        scalar2=0.0, op0=ALU.add, op1=ALU.max,
                     )
-            h_grouped = grouped_pool.tile([P, N, PACK], BF16, align_bytes=64, tag="grouped")
-            regroup(h_grouped[:], h_rows[:], H_VECTOR_COLUMNS)
-            h_codes = h_pool.tile([P, N], U32, align_bytes=64)
-            h_scales = h_pool.tile([P, N], U8, align_bytes=64)
-            quantise(h_grouped[:], h_codes[:], h_scales[:])
-            products = []
+            h_grouped[head] = h_pool.tile(
+                [P, 1, N, PACK], BF16, align_bytes=64, name="h_grouped", tag="h_grouped"
+            )
+            regroup(h_grouped[head][:], h_rows[:], H_VECTOR_COLUMNS)
+
+        second = {}
+
+        def second_layer(head, first_bank):
+            h_codes = h_pool.tile([P, N], U32, align_bytes=64, name="h_codes", tag="h_codes")
+            h_scales = h_pool.tile([P, N], U8, align_bytes=64, name="h_scales", tag="h_scales")
+            quantise(h_grouped[head][:], h_codes[:], h_scales[:])
+            second[head] = []
             for j in range(D_TILES):
                 product = bank(first_bank + j, [P, N], F32, "product")
                 nc.tensor.matmul_mx(
@@ -238,64 +299,65 @@ def tile_infoncemi_pa_k_kernel(
                     start=True,
                     stop=True,
                 )
-                products.append(product)
-            return products
+                second[head].append(product)
 
-        mu_acc = [bank(m, [P, N], F32, "mu_acc") for m in range(PACK)]
-        first_layer(mu_W1, mu_acc)
-        mu_t = second_layer("mu", mu_acc, MU_B1, 0)
-        pos_terms = []
-        neg_terms = []
-        for j in range(D_TILES):
-            pos_term = const.tile([P, N], F32, name="pos_term%d" % j)
+        pos_terms = [term_pool.tile([P, N], F32, name="pos_term%d" % j) for j in range(D_TILES)]
+        neg_terms = [term_pool.tile([P, N], F32, name="neg_term%d" % j) for j in range(D_TILES)]
+
+        def mu_terms(j):
             nc.vector.scalar_tensor_tensor(
-                out=pos_term[:],
-                in0=mu_t[j][:],
-                scalar=bias_column(MU_B2, j),
-                in1=y_t[:, j, :],
-                op0=ALU.add,
-                op1=ALU.subtract,
+                out=pos_terms[j][:], in0=second["mu"][j][:], scalar=bias_column(MU_B2, j),
+                in1=y_t[:, j, :], op0=ALU.add, op1=ALU.subtract,
             )
-            nc.scalar.activation(out=pos_term[:], in_=pos_term[:], func=ACT.Square)
-            neg_term = const.tile([P, N], F32, name="neg_term%d" % j)
             nc.scalar.activation(
-                out=neg_term[:], in_=mu_t[j][:], func=ACT.Square, bias=centre[:, j : j + 1]
+                out=neg_terms[j][:], in_=second["mu"][j][:], func=ACT.Square, bias=centre[:, j : j + 1]
             )
-            pos_terms.append(pos_term)
-            neg_terms.append(neg_term)
+            nc.scalar.activation(out=pos_terms[j][:], in_=pos_terms[j][:], func=ACT.Square)
 
-        lv_acc = [bank(PACK + m, [P, N], F32, "lv_acc") for m in range(PACK)]
-        first_layer(lv_W1, lv_acc)
-        lv_t = second_layer("lv", lv_acc, LV_B1, PACK)
+        mu_epilogue = (
+            lambda: hidden("mu", MU_B1),
+            lambda: second_layer("mu", 0),
+            lambda: (mu_terms(0), mu_terms(1)),
+            lambda: (mu_terms(2), mu_terms(3)),
+        )
+        first_step = PASSES // W1_PASSES_PER_LOAD + EPILOGUE_LAG
+
+        for k in range(len(loads)):
+            regroup_load(k)
+            start_load(k + RAW_BUFS)
+            if k >= 1:
+                quantise_and_multiply(k - 1)
+            if 0 <= k - first_step < len(mu_epilogue):
+                mu_epilogue[k - first_step]()
+        quantise_and_multiply(len(loads) - 1)
+        hidden("lv", LV_B1)
+        second_layer("lv", PACK)
 
         pos_sum = bank(0, [P, N], F32, "pos_sum")
         neg_sum = bank(1, [P, N], F32, "neg_sum")
+
+        def add_up(j, start, stop):
+            nc.tensor.matmul(out=pos_sum[:], lhsT=pos_weight[:], rhs=pos_terms[j][:], start=start, stop=stop)
+            nc.tensor.matmul(out=neg_sum[:], lhsT=neg_weight[:], rhs=neg_terms[j][:], start=start, stop=stop)
+
         for j in range(D_TILES):
             weight = tail_pool.tile([P, N], F32)
             nc.scalar.activation(
-                out=weight[:], in_=lv_t[j][:], func=ACT.Tanh, bias=bias_column(LV_B2, j)
+                out=weight[:], in_=second["lv"][j][:], func=ACT.Tanh, bias=bias_column(LV_B2, j)
             )
             nc.scalar.activation(out=weight[:], in_=weight[:], func=ACT.Exp, scale=-1.0)
-            nc.vector.tensor_tensor(
-                out=pos_terms[j][:], in0=pos_terms[j][:], in1=weight[:], op=ALU.mult
-            )
+            nc.vector.tensor_tensor(out=pos_terms[j][:], in0=pos_terms[j][:], in1=weight[:], op=ALU.mult)
             nc.vector.scalar_tensor_tensor(
-                out=neg_terms[j][:],
-                in0=neg_terms[j][:],
-                scalar=var_y[:, j : j + 1],
-                in1=weight[:],
-                op0=ALU.add,
-                op1=ALU.mult,
+                out=neg_terms[j][:], in0=neg_terms[j][:], scalar=var_y[:, j : j + 1], in1=weight[:],
+                op0=ALU.add, op1=ALU.mult,
             )
-            nc.tensor.matmul(
-                out=pos_sum[:], lhsT=pos_weight[:], rhs=pos_terms[j][:],
-                start=(j == 0), stop=(j == D_TILES - 1),
-            )
-            nc.tensor.matmul(
-                out=neg_sum[:], lhsT=neg_weight[:], rhs=neg_terms[j][:],
-                start=(j == 0), stop=(j == D_TILES - 1),
-            )
-        result = const.tile([P, 2, N], F32)
+            if j < D_TILES - 2:
+                add_up(j, j == 0, False)
+        last = D_TILES - 1
+        nc.vector.tensor_tensor(out=pos_terms[last][:], in0=pos_terms[last][:], in1=pos_terms[last - 1][:], op=ALU.add)
+        nc.vector.tensor_tensor(out=neg_terms[last][:], in0=neg_terms[last][:], in1=neg_terms[last - 1][:], op=ALU.add)
+        add_up(last, False, True)
+        result = term_pool.tile([P, 2, N], F32)
         nc.scalar.copy(out=result[:, 0, :], in_=pos_sum[:])
         nc.vector.tensor_copy(out=result[:, 1, :], in_=neg_sum[:])
         nc.sync.dma_start(out=out_0.rearrange("(o n) -> o n", o=1), in_=result[0:1, 0, :])

@@ -33,7 +33,7 @@ RAW_BUFS = 6
 RUN = 4
 W1_VECTOR_COLUMNS = 256
 H_VECTOR_COLUMNS = 336
-EPILOGUE_LAG = 2
+EPILOGUE_LAG = 4
 
 MU_B1, LV_B1, MU_B2, LV_B2 = 0, 1, 2, 3
 
@@ -104,9 +104,9 @@ def tile_infoncemi_pa_k_kernel(
             head, w1, first, passes = loads[k]
             raw = raw_pool.tile([P, passes, PACK, HID], BF16, name="raw", tag="raw")
             nc.sync.dma_start(
-                out=raw[:].rearrange("p g (u e) h -> p (g u) e h", e=2),
+                out=raw[:],
                 in_=w1[first * K_PASS : (first + passes) * K_PASS, :].rearrange(
-                    "(s p e) h -> p s e h", p=P, e=2
+                    "(g p t) h -> p g t h", p=P, t=PACK
                 ),
             )
             raw_tiles[k] = raw
@@ -150,14 +150,13 @@ def tile_infoncemi_pa_k_kernel(
 
             def x_to_mx(r):
                 for piece in range(X_PIECES):
-                    x_words = x_rows[r, piece][:].bitcast(F32)
+                    x_words = x_rows[r, piece][:].bitcast(F32).rearrange("n (g p u) -> n g u p", p=P, u=2)
                     for pair in range(PIECE_PASSES // 2):
                         xt_ps = bank(piece * (PIECE_PASSES // 2) + pair, [P, 2, 2, P], F32, "xt_ps")
                         for g2 in range(2):
                             for u in range(2):
-                                first = (2 * pair + g2) * (K_PASS // 2) + u * P
                                 nc.tensor.transpose(
-                                    xt_ps[:, g2, u, :], x_words[:, first : first + P], ident_f32[:]
+                                    xt_ps[:, g2, u, :], x_words[:, 2 * pair + g2, u, :], ident_f32[:]
                                 )
                         x_grouped = xg_pool.tile([P, 2, P * PACK], BF16, align_bytes=64)
                         word_view = x_grouped[:].rearrange("p g c -> p (g c)").bitcast(F32)

@@ -26,14 +26,15 @@ BANKS = 8
 
 FLOPS = 2 * (2 * N * X_DIM * HID + 2 * N * HID * Y_DIM)
 
-X_PIECES = 2
-PIECE_PASSES = PASSES // X_PIECES
-W1_PASSES_PER_LOAD = 2
-RAW_BUFS = 6
 RUN = 4
-W1_VECTOR_COLUMNS = 256
-H_VECTOR_COLUMNS = 336
-EPILOGUE_LAG = 4
+X_UNITS = (2, 2, 2, 2, 2, 2, 2, 2)
+MU_UNITS = (1, 1, 2, 2, 2, 2, 2, 2, 2)
+LV_UNITS = (2, 2, 2, 2, 2, 2, 2, 1, 1)
+W_BUFS = 6
+X_BUFS = 3
+W1_VECTOR_COLUMNS = {"mu": 336, "lv": 288}
+W2_VECTOR_COLUMNS = 256
+H_VECTOR_COLUMNS = {"mu": 256, "lv": 336}
 
 MU_B1, LV_B1, MU_B2, LV_B2 = 0, 1, 2, 3
 
@@ -44,7 +45,9 @@ def tile_infoncemi_pa_k_kernel(
     nc = tc.nc
     with ExitStack() as ctx:
         const = ctx.enter_context(tc.tile_pool(name="const", bufs=1))
-        raw_pool = ctx.enter_context(tc.tile_pool(name="raw_pool", bufs=RAW_BUFS))
+        raw_pool = ctx.enter_context(tc.tile_pool(name="raw_pool", bufs=W_BUFS))
+        grouped_pool = ctx.enter_context(tc.tile_pool(name="grouped_pool", bufs=3))
+        wq_pool = ctx.enter_context(tc.tile_pool(name="wq_pool", bufs=5))
         psum = ctx.enter_context(tc.psum_pool(name="psum", bufs=1))
 
         def bank(index, shape, dtype, name):
@@ -70,8 +73,14 @@ def tile_infoncemi_pa_k_kernel(
         nc.vector.memset(pos_weight[:], -0.5)
         neg_weight = const.tile([P, P], F32)
         nc.vector.memset(neg_weight[:], -0.5 / N)
+        ones = const.tile([P, 1], BF16)
+        nc.vector.memset(ones[:], 1.0)
         bias_rows = const.tile([P, P], BF16)
         nc.vector.memset(bias_rows[:], 0.0)
+        for place, vector in enumerate((mu_b1, lv_b1, mu_b2, lv_b2)):
+            nc.scalar.dma_start(
+                out=bias_rows[PACK * place : PACK * (place + 1), :], in_=vector.rearrange("(m p) -> m p", p=P)
+            )
 
         x_codes = const.tile([P, PASSES, N], U32, align_bytes=64)
         x_scales = const.tile([P, PASSES, N], U8, align_bytes=64)
@@ -88,20 +97,18 @@ def tile_infoncemi_pa_k_kernel(
         def bias_column(place, m):
             return bias_cols[:, PACK * place + m : PACK * place + m + 1]
 
-        loads = []
-        for head, w1 in (("mu", mu_W1), ("lv", lv_W1)):
-            for first in range(0, PASSES, W1_PASSES_PER_LOAD):
-                if head == "lv" and first == PASSES - W1_PASSES_PER_LOAD:
-                    for g in range(first, PASSES):
-                        loads.append((head, w1, g, 1))
-                else:
-                    loads.append((head, w1, first, W1_PASSES_PER_LOAD))
+        units = []
+        for head, w1, sizes in (("mu", mu_W1, MU_UNITS), ("lv", lv_W1, LV_UNITS)):
+            first = 0
+            for passes in sizes:
+                units.append((head, w1, first, passes))
+                first += passes
         raw_tiles = {}
+        grouped_tiles = {}
+        w_quantised = {}
 
-        def start_load(k):
-            if k >= len(loads):
-                return
-            head, w1, first, passes = loads[k]
+        def load_w(k):
+            head, w1, first, passes = units[k]
             raw = raw_pool.tile([P, passes, PACK, HID], BF16, name="raw", tag="raw")
             nc.sync.dma_start(
                 out=raw[:],
@@ -111,92 +118,162 @@ def tile_infoncemi_pa_k_kernel(
             )
             raw_tiles[k] = raw
 
-        with ExitStack() as phase1:
-            x_pool = phase1.enter_context(tc.tile_pool(name="x_pool", bufs=ROW_TILES * X_PIECES))
-            xg_pool = phase1.enter_context(tc.tile_pool(name="xg_pool", bufs=4))
-            prep = phase1.enter_context(tc.tile_pool(name="prep", bufs=1))
+        def w_regroup(k):
+            head, w1, first, passes = units[k]
+            grouped_tiles[k] = grouped_pool.tile(
+                [P, passes, HID, PACK], BF16, align_bytes=64, name="grouped", tag="grouped"
+            )
+            regroup(grouped_tiles[k][:], raw_tiles[k][:], W1_VECTOR_COLUMNS[head])
 
-            for place, vector in enumerate((mu_b1, lv_b1, mu_b2, lv_b2)):
-                nc.scalar.dma_start(
-                    out=bias_rows[PACK * place : PACK * (place + 1), :],
-                    in_=vector.rearrange("(m p) -> m p", p=P),
+        def w_quantise(k):
+            head, w1, first, passes = units[k]
+            w_codes = wq_pool.tile([P, passes * HID], U32, align_bytes=64, name="w_codes", tag="w_codes")
+            w_scales = wq_pool.tile([P, passes * HID], U8, align_bytes=64, name="w_scales", tag="w_scales")
+            quantise(grouped_tiles[k][:], w_codes[:], w_scales[:])
+            for g2 in range(passes):
+                cols = slice(g2 * HID, (g2 + 1) * HID)
+                w_quantised[head, first + g2] = (w_codes[:, cols], w_scales[:, cols])
+
+        acc = {"mu": [bank(m, [P, N], F32, "mu_acc") for m in range(PACK)]}
+
+        def multiply(head, g):
+            w_codes, w_scales = w_quantised[head, g]
+            for m in range(PACK):
+                cols = slice(m * P, (m + 1) * P)
+                nc.tensor.matmul_mx(
+                    out=acc[head][m][:],
+                    lhsT=w_codes[:, cols].bitcast(FP8X4),
+                    lhsT_scale=w_scales[:, cols],
+                    rhs=x_codes[:, g, :].bitcast(FP8X4),
+                    rhs_scale=x_scales[:, g, :],
+                    start=(g == 0),
+                    stop=(g == PASSES - 1),
                 )
-            x_rows = {}
 
-            def load_x(r):
-                for piece in range(X_PIECES):
-                    x_rows[r, piece] = x_pool.tile([P, X_DIM // X_PIECES], BF16, name="x_rows", tag="x_rows")
-                    cols = slice(piece * X_DIM // X_PIECES, (piece + 1) * X_DIM // X_PIECES)
-                    nc.sync.dma_start(out=x_rows[r, piece][:], in_=x_samples[r * P : (r + 1) * P, cols])
+        load_queue = []
+        buffers_free = {"w": W_BUFS, "x": X_BUFS, "w2": 1}
 
+        def issue_loads():
+            while load_queue and buffers_free.get(load_queue[0][0], 1) > 0:
+                kind, load = load_queue[0]
+                if kind in buffers_free:
+                    buffers_free[kind] -= 1
+                load()
+                load_queue.remove(load_queue[0])
+
+        mu_units = len(MU_UNITS)
+        x_firsts = [sum(X_UNITS[:k]) for k in range(len(X_UNITS))]
+        ctx.enter_context(tc.manual_schedule())
+
+        if True:
+            x_pool = ctx.enter_context(tc.tile_pool(name="x_pool", bufs=X_BUFS))
+            xg_pool = ctx.enter_context(tc.tile_pool(name="xg_pool", bufs=2))
+            prep = ctx.enter_context(tc.tile_pool(name="prep", bufs=1))
+
+            x_words = {}
             w2_raw = {}
+            y_rows = prep.tile([P, ROW_TILES, Y_DIM], BF16)
+
+            def load_x(first, passes):
+                chunk = x_pool.tile([P, ROW_TILES, passes * K_PASS], BF16, name="x_chunk", tag="x_chunk")
+                nc.sync.dma_start(
+                    out=chunk[:],
+                    in_=x_samples[:, first * K_PASS : (first + passes) * K_PASS].rearrange(
+                        "(r p) k -> p r k", p=P
+                    ),
+                )
+                words = chunk[:].rearrange("p r k -> p (r k)").bitcast(F32).rearrange(
+                    "n (r g p u) -> n g r u p", r=ROW_TILES, p=P, u=2
+                )
+                for g in range(passes):
+                    x_words[first + g] = words[:, g]
 
             def load_w2(head, w2):
-                w2_raw[head] = prep.tile([P, 1, PACK, Y_DIM], BF16, name="w2_raw_" + head)
-                nc.sync.dma_start(
-                    out=w2_raw[head][:, 0], in_=w2.rearrange("(t p) d -> p t d", p=P)
+                w2_raw[head] = prep.tile([P, 1, PACK, Y_DIM], BF16, name="w2_raw", tag="w2_raw")
+                nc.sync.dma_start(out=w2_raw[head][:, 0], in_=w2.rearrange("(t p) d -> p t d", p=P))
+
+            def load_y():
+                nc.sync.dma_start(out=y_rows[:], in_=y_samples.rearrange("(r p) d -> p r d", p=P))
+
+            spare_banks = []
+
+            def spare_bank(shape, dtype, name):
+                spare_banks.append(name)
+                return bank(PACK + len(spare_banks) % PACK, shape, dtype, name)
+
+            x_grouped = {}
+
+            def x_transpose(k):
+                first, passes = x_firsts[k], X_UNITS[k]
+                x_grouped[k] = xg_pool.tile(
+                    [P, passes * N * PACK], BF16, align_bytes=64, name="x_grouped", tag="x_grouped"
                 )
-
-            y_rows = prep.tile([P, ROW_TILES, Y_DIM], BF16)
-            load_x(0)
-            nc.sync.dma_start(out=y_rows[:], in_=y_samples.rearrange("(r p) d -> p r d", p=P))
-            load_x(1)
-            load_w2("mu", mu_W2)
-            load_x(2)
-            load_w2("lv", lv_W2)
-            load_x(3)
-            for k in range(RAW_BUFS):
-                start_load(k)
-
-            def x_to_mx(r):
-                for piece in range(X_PIECES):
-                    x_words = x_rows[r, piece][:].bitcast(F32).rearrange("n (g p u) -> n g u p", p=P, u=2)
-                    for pair in range(PIECE_PASSES // 2):
-                        xt_ps = bank(piece * (PIECE_PASSES // 2) + pair, [P, 2, 2, P], F32, "xt_ps")
-                        for g2 in range(2):
+                word_view = x_grouped[k][:].bitcast(F32).rearrange(
+                    "p (g r n u) -> p g r n u", g=passes, r=ROW_TILES, u=2
+                )
+                for g2 in range(passes):
+                    for half in range(2):
+                        xt_ps = spare_bank([P, 2, 2, P], F32, "xt_ps")
+                        for r2 in range(2):
                             for u in range(2):
                                 nc.tensor.transpose(
-                                    xt_ps[:, g2, u, :], x_words[:, 2 * pair + g2, u, :], ident_f32[:]
+                                    xt_ps[:, r2, u, :], x_words[first + g2][:, 2 * half + r2, u, :], ident_f32[:]
                                 )
-                        x_grouped = xg_pool.tile([P, 2, P * PACK], BF16, align_bytes=64)
-                        word_view = x_grouped[:].rearrange("p g c -> p (g c)").bitcast(F32)
-                        copy_out = word_view.rearrange("p (g n u) -> p g n u", g=2, u=2)
-                        copy_in = xt_ps[:].rearrange("p g u n -> p g n u")
-                        if pair % 4 == 3:
-                            nc.vector.tensor_copy(out=copy_out, in_=copy_in)
-                        else:
-                            nc.scalar.copy(out=copy_out, in_=copy_in)
-                        for g2 in range(2):
-                            g = piece * PIECE_PASSES + 2 * pair + g2
-                            nc.vector.quantize_mx(
-                                out=x_codes[:, g, r * P : (r + 1) * P].bitcast(FP8X4),
-                                scales=x_scales[:, g, r * P : (r + 1) * P],
-                                in_=x_grouped[:, g2, :],
-                            )
+                        nc.scalar.copy(
+                            out=word_view[:, g2, 2 * half : 2 * half + 2],
+                            in_=xt_ps[:].rearrange("p r u n -> p r n u"),
+                        )
 
-            def y_and_biases():
-                bias_ps = bank(4, [P, P], BF16, "bias_ps")
+            def x_quantise(k):
+                first, passes = x_firsts[k], X_UNITS[k]
+                nc.vector.quantize_mx(
+                    out=x_codes[:, first : first + passes, :].rearrange("p g n -> p (g n)").bitcast(FP8X4),
+                    scales=x_scales[:, first : first + passes, :].rearrange("p g n -> p (g n)"),
+                    in_=x_grouped[k][:],
+                )
+
+            def biases():
+                bias_ps = spare_bank([P, P], BF16, "bias_ps")
                 nc.tensor.transpose(bias_ps[:], bias_rows[:], ident_bf16[:])
                 nc.vector.tensor_copy(out=bias_cols[:], in_=bias_ps[:, 0 : 4 * PACK])
-                y_squares = prep.tile([P, D_TILES, N], BF16)
-                sum_y = prep.tile([P, D_TILES], F32)
-                sum_y2 = prep.tile([P, D_TILES], F32)
+
+            sum_y2 = prep.tile([P, D_TILES], F32)
+            sums = {}
+
+            def y_sums():
+                sums["y"] = spare_bank([P, D_TILES], F32, "sum_ps")
+                sums["gram"] = spare_bank([P, D_TILES, P], F32, "gram_ps")
                 for j in range(D_TILES):
-                    yt_ps = bank(j, [P, N], BF16, "yt_ps")
                     for r in range(ROW_TILES):
-                        nc.tensor.transpose(
-                            yt_ps[:, r * P : (r + 1) * P], y_rows[:, r, j * P : (j + 1) * P], ident_bf16[:]
+                        y_block = y_rows[:, r, j * P : (j + 1) * P]
+                        nc.tensor.matmul(
+                            out=sums["gram"][:, j, :], lhsT=y_block, rhs=y_block, start=(r == 0), stop=(r == ROW_TILES - 1)
                         )
-                    nc.scalar.activation(
-                        out=y_t[:, j, :], in_=yt_ps[:], func=ACT.Copy, accum_out=sum_y[:, j : j + 1]
+                    for r in range(ROW_TILES):
+                        nc.tensor.matmul(
+                            out=sums["y"][:, j : j + 1], lhsT=y_rows[:, r, j * P : (j + 1) * P], rhs=ones[:],
+                            start=(r == 0), stop=(r == ROW_TILES - 1),
+                        )
+
+            def y_diagonal(j):
+                diagonal = prep.tile([P, P], F32, name="diagonal", tag="diagonal")
+                nc.vector.scalar_tensor_tensor(
+                    out=diagonal[:], in0=sums["gram"][:, j, :], scalar=1.0, in1=ident_f32[:],
+                    op0=ALU.mult, op1=ALU.mult, accum_out=sum_y2[:, j : j + 1],
+                )
+
+            def y_transpose(j):
+                yt_ps = spare_bank([P, N], BF16, "yt_ps")
+                for r in range(ROW_TILES):
+                    nc.tensor.transpose(
+                        yt_ps[:, r * P : (r + 1) * P], y_rows[:, r, j * P : (j + 1) * P], ident_bf16[:]
                     )
-                    nc.scalar.activation(
-                        out=y_squares[:, j, :], in_=y_t[:, j, :], func=ACT.Square,
-                        accum_out=sum_y2[:, j : j + 1],
-                    )
+                nc.scalar.copy(out=y_t[:, j, :], in_=yt_ps[:])
+
+            def y_moments():
                 mean_y = prep.tile([P, D_TILES], F32)
                 nc.vector.tensor_scalar(
-                    out=mean_y[:], in0=sum_y[:], scalar1=1.0 / N, scalar2=None, op0=ALU.mult
+                    out=mean_y[:], in0=sums["y"][:], scalar1=1.0 / N, scalar2=None, op0=ALU.mult
                 )
                 mean_sq = prep.tile([P, D_TILES], F32)
                 nc.vector.tensor_tensor(out=mean_sq[:], in0=mean_y[:], in1=mean_y[:], op=ALU.mult)
@@ -209,155 +286,234 @@ def tile_infoncemi_pa_k_kernel(
                     op=ALU.subtract,
                 )
 
-            def w2_to_mx(head):
-                w2_grouped = prep.tile([P, 1, Y_DIM, PACK], BF16, align_bytes=64, name="w2_grouped_" + head)
-                regroup(w2_grouped[:], w2_raw[head][:], W1_VECTOR_COLUMNS)
-                quantise(w2_grouped[:], w2_codes[head][:], w2_scales[head][:])
+            w2_grouped = {}
 
-            x_to_mx(0)
-            y_and_biases()
-            x_to_mx(1)
-            w2_to_mx("mu")
-            x_to_mx(2)
-            w2_to_mx("lv")
-            x_to_mx(3)
+            def w2_regroup(head):
+                w2_grouped[head] = prep.tile(
+                    [P, 1, Y_DIM, PACK], BF16, align_bytes=64, name="w2_grouped", tag="w2_grouped"
+                )
+                regroup(w2_grouped[head][:], w2_raw[head][:], W2_VECTOR_COLUMNS)
 
-        grouped_pool = ctx.enter_context(tc.tile_pool(name="grouped_pool", bufs=3, reuse_waits="tile"))
-        wq_pool = ctx.enter_context(tc.tile_pool(name="wq_pool", bufs=3, reuse_waits="tile"))
-        h_pool = ctx.enter_context(tc.tile_pool(name="h_pool", bufs=1, reuse_waits="tile"))
-        term_pool = ctx.enter_context(tc.tile_pool(name="term_pool", bufs=1, reuse_waits="tile"))
-        tail_pool = ctx.enter_context(tc.tile_pool(name="tail_pool", bufs=3, reuse_waits="tile"))
+            def w2_quantise(head):
+                quantise(w2_grouped[head][:], w2_codes[head][:], w2_scales[head][:])
 
-        acc = {
-            "mu": [bank(m, [P, N], F32, "mu_acc") for m in range(PACK)],
-            "lv": [bank(PACK + m, [P, N], F32, "lv_acc") for m in range(PACK)],
-        }
-        grouped_tiles = {}
+            def y_stage_1():
+                for j in range(D_TILES):
+                    y_transpose(j)
+                y_sums()
 
-        def regroup_load(k):
-            passes = loads[k][3]
-            grouped_tiles[k] = grouped_pool.tile(
-                [P, passes, HID, PACK], BF16, align_bytes=64, name="grouped", tag="grouped"
-            )
-            regroup(grouped_tiles[k][:], raw_tiles[k][:], W1_VECTOR_COLUMNS)
+            def y_stage_2():
+                for j in range(D_TILES):
+                    y_diagonal(j)
+                y_moments()
 
-        def quantise_and_multiply(k):
-            head, w1, first, passes = loads[k]
-            w_codes = wq_pool.tile([P, passes * HID], U32, align_bytes=64, name="w_codes", tag="w_codes")
-            w_scales = wq_pool.tile([P, passes * HID], U8, align_bytes=64, name="w_scales", tag="w_scales")
-            quantise(grouped_tiles[k][:], w_codes[:], w_scales[:])
-            for g2 in range(passes):
-                g = first + g2
-                for m in range(PACK):
-                    cols = slice(g2 * HID + m * P, g2 * HID + (m + 1) * P)
-                    nc.tensor.matmul_mx(
-                        out=acc[head][m][:],
-                        lhsT=w_codes[:, cols].bitcast(FP8X4),
-                        lhsT_scale=w_scales[:, cols],
-                        rhs=x_codes[:, g, :].bitcast(FP8X4),
-                        rhs_scale=x_scales[:, g, :],
-                        start=(g == 0),
-                        stop=(g == PASSES - 1),
-                    )
+            def release(kind):
+                buffers_free[kind] += 1
 
+            items = {"y": (load_y, y_stage_1, y_stage_2, ())}
+            for head, w2 in (("mu", mu_W2), ("lv", lv_W2)):
+                items["w2", head] = (
+                    lambda head=head, w2=w2: load_w2(head, w2),
+                    lambda head=head: (w2_regroup(head), release("w2")),
+                    lambda head=head: w2_quantise(head),
+                    (),
+                )
+            for k in range(len(X_UNITS)):
+                items["x", k] = (
+                    lambda k=k: load_x(x_firsts[k], X_UNITS[k]),
+                    lambda k=k: (x_transpose(k), release("x")),
+                    lambda k=k: x_quantise(k),
+                    [("x", x_firsts[k] + g) for g in range(X_UNITS[k])],
+                )
+            for k in range(len(units)):
+                items["w", k] = (
+                    lambda k=k: load_w(k),
+                    lambda k=k: (w_regroup(k), release("w")),
+                    lambda k=k: w_quantise(k),
+                    [(units[k][0], units[k][2] + g) for g in range(units[k][3])],
+                )
+        h_pool = ctx.enter_context(tc.tile_pool(name="h_pool", bufs=1))
+        term_pool = ctx.enter_context(tc.tile_pool(name="term_pool", bufs=1))
+        tail_pool = ctx.enter_context(tc.tile_pool(name="tail_pool", bufs=4))
+
+        h_rows = {}
         h_grouped = {}
 
-        def hidden(head, b1_place):
-            h_rows = h_pool.tile([P, 1, PACK, N], BF16, name="h_rows", tag="h_rows")
+        def hidden(head, b1_place, part):
+            if head not in h_rows:
+                h_rows[head] = h_pool.tile([P, 1, PACK, N], BF16, name="h_rows", tag="h_rows")
             for m in range(PACK):
                 if m % 2 == 0:
                     nc.scalar.activation(
-                        out=h_rows[:, 0, m, :], in_=acc[head][m][:], func=ACT.Relu,
+                        out=h_rows[head][:, 0, m, part], in_=acc[head][m][:, part], func=ACT.Relu,
                         bias=bias_column(b1_place, m),
                     )
                 else:
                     nc.vector.tensor_scalar(
-                        out=h_rows[:, 0, m, :], in0=acc[head][m][:], scalar1=bias_column(b1_place, m),
+                        out=h_rows[head][:, 0, m, part], in0=acc[head][m][:, part], scalar1=bias_column(b1_place, m),
                         scalar2=0.0, op0=ALU.add, op1=ALU.max,
                     )
-            h_grouped[head] = h_pool.tile(
-                [P, 1, N, PACK], BF16, align_bytes=64, name="h_grouped", tag="h_grouped"
+
+        def hidden_regroup(head, part):
+            if head not in h_grouped:
+                h_grouped[head] = h_pool.tile(
+                    [P, 1, N, PACK], BF16, align_bytes=64, name="h_grouped", tag="h_grouped"
+                )
+            samples = part.stop - part.start
+            regroup(
+                h_grouped[head][:, :, part, :], h_rows[head][:, :, :, part],
+                H_VECTOR_COLUMNS[head] * samples // N // (2 * RUN) * (2 * RUN),
             )
-            regroup(h_grouped[head][:], h_rows[:], H_VECTOR_COLUMNS)
+
+        h_quantised = {}
+
+        def hidden_quantise(head, part):
+            if head not in h_quantised:
+                h_quantised[head] = (
+                    h_pool.tile([P, N], U32, align_bytes=64, name="h_codes", tag="h_codes"),
+                    h_pool.tile([P, N], U8, align_bytes=64, name="h_scales", tag="h_scales"),
+                )
+            h_codes, h_scales = h_quantised[head]
+            quantise(h_grouped[head][:, :, part, :], h_codes[:, part], h_scales[:, part])
 
         second = {}
 
-        def second_layer(head, first_bank):
-            h_codes = h_pool.tile([P, N], U32, align_bytes=64, name="h_codes", tag="h_codes")
-            h_scales = h_pool.tile([P, N], U8, align_bytes=64, name="h_scales", tag="h_scales")
-            quantise(h_grouped[head][:], h_codes[:], h_scales[:])
-            second[head] = []
-            for j in range(D_TILES):
-                product = bank(first_bank + j, [P, N], F32, "product")
-                nc.tensor.matmul_mx(
-                    out=product[:],
-                    lhsT=w2_codes[head][:, j * P : (j + 1) * P].bitcast(FP8X4),
-                    lhsT_scale=w2_scales[head][:, j * P : (j + 1) * P],
-                    rhs=h_codes[:].bitcast(FP8X4),
-                    rhs_scale=h_scales[:],
-                    start=True,
-                    stop=True,
-                )
-                second[head].append(product)
+        def second_layer(head, j, part, bank_index):
+            h_codes, h_scales = h_quantised[head]
+            product = bank(bank_index, [P, part.stop - part.start], F32, "product")
+            nc.tensor.matmul_mx(
+                out=product[:],
+                lhsT=w2_codes[head][:, j * P : (j + 1) * P].bitcast(FP8X4),
+                lhsT_scale=w2_scales[head][:, j * P : (j + 1) * P],
+                rhs=h_codes[:, part].bitcast(FP8X4),
+                rhs_scale=h_scales[:, part],
+                start=True,
+                stop=True,
+            )
+            second[head, j, part.start] = product
 
-        pos_terms = [term_pool.tile([P, N], F32, name="pos_term%d" % j) for j in range(D_TILES)]
-        neg_terms = [term_pool.tile([P, N], F32, name="neg_term%d" % j) for j in range(D_TILES)]
+        everyone = slice(0, N)
+        terms = {}
+
+        def start_terms():
+            for sign in ("pos", "neg"):
+                terms[sign] = x_pool.tile([P, D_TILES, N], F32, name="terms", tag="x_chunk")
 
         def mu_terms(j):
             nc.vector.scalar_tensor_tensor(
-                out=pos_terms[j][:], in0=second["mu"][j][:], scalar=bias_column(MU_B2, j),
+                out=terms["pos"][:, j, :], in0=second["mu", j, 0][:], scalar=bias_column(MU_B2, j),
                 in1=y_t[:, j, :], op0=ALU.add, op1=ALU.subtract,
             )
             nc.scalar.activation(
-                out=neg_terms[j][:], in_=second["mu"][j][:], func=ACT.Square, bias=centre[:, j : j + 1]
+                out=terms["neg"][:, j, :], in_=second["mu", j, 0][:], func=ACT.Square, bias=centre[:, j : j + 1]
             )
-            nc.scalar.activation(out=pos_terms[j][:], in_=pos_terms[j][:], func=ACT.Square)
 
-        mu_epilogue = (
-            lambda: hidden("mu", MU_B1),
-            lambda: second_layer("mu", 0),
-            lambda: (mu_terms(0), mu_terms(1)),
-            lambda: (mu_terms(2), mu_terms(3)),
+        def pos_square(j):
+            nc.scalar.activation(out=terms["pos"][:, j, :], in_=terms["pos"][:, j, :], func=ACT.Square)
+
+        epilogue = (
+            (lambda: hidden("mu", MU_B1, everyone), lambda: hidden_regroup("mu", everyone)),
+            (
+                lambda: hidden_quantise("mu", everyone),
+                lambda: [second_layer("mu", j, everyone, j) for j in range(D_TILES)],
+            ),
+            (lambda: (start_terms(), mu_terms(0)), lambda: (mu_terms(1), pos_square(0))),
+            (lambda: pos_square(1), lambda: mu_terms(2)),
+            (lambda: (pos_square(2), mu_terms(3)), lambda: pos_square(3)),
         )
-        first_step = PASSES // W1_PASSES_PER_LOAD + EPILOGUE_LAG
+        for e in range(len(epilogue)):
+            items["mu", e] = (None,) + epilogue[e] + ((),)
 
-        for k in range(len(loads)):
-            regroup_load(k)
-            start_load(k + RAW_BUFS)
-            if k >= 1:
-                quantise_and_multiply(k - 1)
-            if 0 <= k - first_step < len(mu_epilogue):
-                mu_epilogue[k - first_step]()
-        quantise_and_multiply(len(loads) - 1)
-        hidden("lv", LV_B1)
-        second_layer("lv", PACK)
+        order = (("w", 0), ("w", 1), ("x", 0), ("w", 2), "y", ("w", 3), ("x", 1), ("w", 4), ("x", 2), ("w", 5), ("x", 3), ("w", 6), ("w2", "mu"), ("x", 4), ("w", 7), ("w", 8), ("x", 5), ("w", 9), ("w2", "lv"), ("x", 6), ("w", 10), ("x", 7), ("w", 11), ("w", 12), ("w", 13), ("mu", 0), ("w", 14), ("mu", 1), ("w", 15), ("mu", 2), ("w", 16), ("mu", 3), ("w", 17), ("mu", 4))
+        load_queue += [(name[0], items[name][0]) for name in order if items[name][0]]
+        issue_loads()
+        biases()
+        done = set()
+        multiplied = {"mu": 0, "lv": 0}
+        previous = None
+        for name in order:
+            load, stage_1, stage_2, ready = items[name]
+            stage_1()
+            issue_loads()
+            if previous:
+                previous[0]()
+            for head in ("mu", "lv"):
+                while (head, multiplied[head]) in done and ("x", multiplied[head] if head == "mu" else PASSES - 1) in done:
+                    if head == "lv" and multiplied["lv"] == 0:
+                        acc["lv"] = [bank(PACK + m, [P, N], F32, "lv_acc") for m in range(PACK)]
+                    multiply(head, multiplied[head])
+                    multiplied[head] += 1
+            if previous:
+                done.update(previous[1])
+            previous = (stage_2, ready)
+        previous[0]()
+        for g in range(multiplied["lv"], PASSES):
+            multiply("lv", g)
 
-        pos_sum = bank(0, [P, N], F32, "pos_sum")
-        neg_sum = bank(1, [P, N], F32, "neg_sum")
+        halves = (slice(0, N // 2), slice(N // 2, N))
+        sums_ps = {}
 
-        def add_up(j, start, stop):
-            nc.tensor.matmul(out=pos_sum[:], lhsT=pos_weight[:], rhs=pos_terms[j][:], start=start, stop=stop)
-            nc.tensor.matmul(out=neg_sum[:], lhsT=neg_weight[:], rhs=neg_terms[j][:], start=start, stop=stop)
+        weight = {}
 
-        for j in range(D_TILES):
-            weight = tail_pool.tile([P, N], F32)
+        def tanh(j, part):
+            weight[j, part.start] = tail_pool.tile([P, part.stop - part.start], F32, name="weight", tag="weight")
             nc.scalar.activation(
-                out=weight[:], in_=second["lv"][j][:], func=ACT.Tanh, bias=bias_column(LV_B2, j)
+                out=weight[j, part.start][:], in_=second["lv", j, part.start][:], func=ACT.Tanh, bias=bias_column(LV_B2, j)
             )
-            nc.scalar.activation(out=weight[:], in_=weight[:], func=ACT.Exp, scale=-1.0)
-            nc.vector.tensor_tensor(out=pos_terms[j][:], in0=pos_terms[j][:], in1=weight[:], op=ALU.mult)
+
+        def weight_terms(j, part):
+            w = weight[j, part.start]
+            nc.scalar.activation(out=w[:], in_=w[:], func=ACT.Exp, scale=-1.0)
+            nc.vector.tensor_tensor(
+                out=terms["pos"][:, j, part], in0=terms["pos"][:, j, part], in1=w[:], op=ALU.mult
+            )
             nc.vector.scalar_tensor_tensor(
-                out=neg_terms[j][:], in0=neg_terms[j][:], scalar=var_y[:, j : j + 1], in1=weight[:],
+                out=terms["neg"][:, j, part], in0=terms["neg"][:, j, part], scalar=var_y[:, j : j + 1], in1=w[:],
                 op0=ALU.add, op1=ALU.mult,
             )
-            if j < D_TILES - 2:
-                add_up(j, j == 0, False)
-        last = D_TILES - 1
-        nc.vector.tensor_tensor(out=pos_terms[last][:], in0=pos_terms[last][:], in1=pos_terms[last - 1][:], op=ALU.add)
-        nc.vector.tensor_tensor(out=neg_terms[last][:], in0=neg_terms[last][:], in1=neg_terms[last - 1][:], op=ALU.add)
-        add_up(last, False, True)
+
+        def add_up(j, part, start, stop):
+            for i, (sign, weights) in enumerate((("pos", pos_weight), ("neg", neg_weight))):
+                nc.tensor.matmul(
+                    out=sums_ps[i, part.start][:], lhsT=weights[:], rhs=terms[sign][:, j, part], start=start, stop=stop
+                )
+
+        def join(j, part):
+            for sign in ("pos", "neg"):
+                nc.vector.tensor_tensor(
+                    out=terms[sign][:, j, part], in0=terms[sign][:, j, part], in1=terms[sign][:, j - 1, part], op=ALU.add
+                )
+
+        for h, part in enumerate(halves):
+            hidden("lv", LV_B1, part)
+        for h, part in enumerate(halves):
+            hidden_regroup("lv", part)
+            hidden_quantise("lv", part)
+            for j in range(D_TILES):
+                second_layer("lv", j, part, PACK * h + j)
         result = term_pool.tile([P, 2, N], F32)
-        nc.scalar.copy(out=result[:, 0, :], in_=pos_sum[:])
-        nc.vector.tensor_copy(out=result[:, 1, :], in_=neg_sum[:])
-        nc.sync.dma_start(out=out_0.rearrange("(o n) -> o n", o=1), in_=result[0:1, 0, :])
-        nc.sync.dma_start(out=out_1.rearrange("(o n) -> o n", o=1), in_=result[0:1, 1, :])
+        last = D_TILES - 1
+        for h, part in enumerate(halves):
+            for i in range(2):
+                sums_ps[i, part.start] = bank(2 * h + i, [P, N // 2], F32, "sum_ps")
+        pieces = [(j, part) for part in halves for j in range(D_TILES)]
+
+        def store(part):
+            nc.scalar.copy(out=result[:, 0, part], in_=sums_ps[0, part.start][:])
+            nc.vector.tensor_copy(out=result[:, 1, part], in_=sums_ps[1, part.start][:])
+            nc.sync.dma_start(out=out_0.rearrange("(o n) -> o n", o=1)[:, part], in_=result[0:1, 0, part])
+            nc.sync.dma_start(out=out_1.rearrange("(o n) -> o n", o=1)[:, part], in_=result[0:1, 1, part])
+
+        tanh(*pieces[0])
+        for k, (j, part) in enumerate(pieces):
+            if k + 1 < len(pieces):
+                tanh(*pieces[k + 1])
+            weight_terms(j, part)
+            if j < D_TILES - 2:
+                add_up(j, part, j == 0, False)
+            if j == last:
+                join(last, part)
+                add_up(last, part, False, True)
+            if k == len(pieces) - 1 - 1:
+                store(halves[0])
+        store(halves[1])

@@ -32,7 +32,7 @@ MU_UNITS = (1, 1, 2, 2, 2, 2, 2, 2, 2)
 LV_UNITS = (2, 2, 2, 2, 2, 2, 2, 1, 1)
 W_BUFS = 6
 X_BUFS = 3
-W1_VECTOR_COLUMNS = {"mu": 336, "lv": 288}
+W1_VECTOR_COLUMNS = {"mu": 336, "lv": 240}
 W2_VECTOR_COLUMNS = 256
 H_VECTOR_COLUMNS = {"mu": 256, "lv": 336}
 
@@ -163,7 +163,6 @@ def tile_infoncemi_pa_k_kernel(
 
         mu_units = len(MU_UNITS)
         x_firsts = [sum(X_UNITS[:k]) for k in range(len(X_UNITS))]
-        ctx.enter_context(tc.manual_schedule())
 
         if True:
             x_pool = ctx.enter_context(tc.tile_pool(name="x_pool", bufs=X_BUFS))
@@ -298,6 +297,7 @@ def tile_infoncemi_pa_k_kernel(
                 quantise(w2_grouped[head][:], w2_codes[head][:], w2_scales[head][:])
 
             def y_stage_1():
+                biases()
                 for j in range(D_TILES):
                     y_transpose(j)
                 y_sums()
@@ -427,7 +427,6 @@ def tile_infoncemi_pa_k_kernel(
         order = (("w", 0), ("w", 1), ("x", 0), ("w", 2), "y", ("w", 3), ("x", 1), ("w", 4), ("x", 2), ("w", 5), ("x", 3), ("w", 6), ("w2", "mu"), ("x", 4), ("w", 7), ("w", 8), ("x", 5), ("w", 9), ("w2", "lv"), ("x", 6), ("w", 10), ("x", 7), ("w", 11), ("w", 12), ("w", 13), ("mu", 0), ("w", 14), ("mu", 1), ("w", 15), ("mu", 2), ("w", 16), ("mu", 3), ("w", 17), ("mu", 4))
         load_queue += [(name[0], items[name][0]) for name in order if items[name][0]]
         issue_loads()
-        biases()
         done = set()
         multiplied = {"mu": 0, "lv": 0}
         previous = None

@@ -32,9 +32,9 @@ MU_UNITS = (1, 1, 2, 2, 2, 2, 2, 2, 2)
 LV_UNITS = (2, 2, 2, 2, 2, 2, 2, 1, 1)
 W_BUFS = 6
 X_BUFS = 3
-W1_VECTOR_COLUMNS = {"mu": 336, "lv": 240}
+W1_VECTOR_COLUMNS = {"mu": 304, "lv": 240}
 W2_VECTOR_COLUMNS = 256
-H_VECTOR_COLUMNS = {"mu": 256, "lv": 336}
+H_VECTOR_COLUMNS = {"mu": 304, "lv": 336}
 
 MU_B1, LV_B1, MU_B2, LV_B2 = 0, 1, 2, 3
 
@@ -47,7 +47,7 @@ def tile_infoncemi_pa_k_kernel(
         const = ctx.enter_context(tc.tile_pool(name="const", bufs=1))
         raw_pool = ctx.enter_context(tc.tile_pool(name="raw_pool", bufs=W_BUFS))
         grouped_pool = ctx.enter_context(tc.tile_pool(name="grouped_pool", bufs=3))
-        wq_pool = ctx.enter_context(tc.tile_pool(name="wq_pool", bufs=5))
+        wq_pool = ctx.enter_context(tc.tile_pool(name="wq_pool", bufs=8))
         psum = ctx.enter_context(tc.psum_pool(name="psum", bufs=1))
 
         def bank(index, shape, dtype, name):
@@ -134,7 +134,7 @@ def tile_infoncemi_pa_k_kernel(
                 cols = slice(g2 * HID, (g2 + 1) * HID)
                 w_quantised[head, first + g2] = (w_codes[:, cols], w_scales[:, cols])
 
-        acc = {"mu": [bank(m, [P, N], F32, "mu_acc") for m in range(PACK)]}
+        acc = {}
 
         def multiply(head, g):
             w_codes, w_scales = w_quantised[head, g]
@@ -198,7 +198,7 @@ def tile_infoncemi_pa_k_kernel(
 
             def spare_bank(shape, dtype, name):
                 spare_banks.append(name)
-                return bank(PACK + len(spare_banks) % PACK, shape, dtype, name)
+                return bank(len(spare_banks), shape, dtype, name)
 
             x_grouped = {}
 
@@ -424,7 +424,7 @@ def tile_infoncemi_pa_k_kernel(
         for e in range(len(epilogue)):
             items["mu", e] = (None,) + epilogue[e] + ((),)
 
-        order = (("w", 0), ("w", 1), ("x", 0), ("w", 2), "y", ("w", 3), ("x", 1), ("w", 4), ("x", 2), ("w", 5), ("x", 3), ("w", 6), ("w2", "mu"), ("x", 4), ("w", 7), ("w", 8), ("x", 5), ("w", 9), ("w2", "lv"), ("x", 6), ("w", 10), ("x", 7), ("w", 11), ("w", 12), ("w", 13), ("mu", 0), ("w", 14), ("mu", 1), ("w", 15), ("mu", 2), ("w", 16), ("mu", 3), ("w", 17), ("mu", 4))
+        order = (("w", 0), ("w", 1), ("x", 0), ("x", 1), "y", ("w", 2), ("x", 2), ("x", 3), ("w", 3), ("x", 4), ("x", 5), ("w", 4), ("x", 6), ("x", 7), ("w2", "mu"), ("w", 5), ("w", 6), ("w", 7), ("w", 8), ("w2", "lv"), ("w", 9), ("w", 10), ("w", 11), ("w", 12), ("w", 13), ("mu", 0), ("w", 14), ("mu", 1), ("w", 15), ("mu", 2), ("w", 16), ("mu", 3), ("w", 17), ("mu", 4))
         load_queue += [(name[0], items[name][0]) for name in order if items[name][0]]
         issue_loads()
         done = set()
@@ -437,9 +437,10 @@ def tile_infoncemi_pa_k_kernel(
             if previous:
                 previous[0]()
             for head in ("mu", "lv"):
-                while (head, multiplied[head]) in done and ("x", multiplied[head] if head == "mu" else PASSES - 1) in done:
-                    if head == "lv" and multiplied["lv"] == 0:
-                        acc["lv"] = [bank(PACK + m, [P, N], F32, "lv_acc") for m in range(PACK)]
+                while (head, multiplied[head]) in done and ("x", PASSES - 1) in done:
+                    if multiplied[head] == 0:
+                        first_bank = PACK * (head == "lv")
+                        acc[head] = [bank(first_bank + m, [P, N], F32, "acc") for m in range(PACK)]
                     multiply(head, multiplied[head])
                     multiplied[head] += 1
             if previous:

@@ -27,7 +27,9 @@ BANKS = 8
 FLOPS = 2 * (2 * N * X_DIM * HID + 2 * N * HID * Y_DIM)
 
 RUN = 4
-X_UNITS = (2, 2, 2, 2, 2, 2, 2, 2)
+X_PIECES = 2
+PIECE_PASSES = PASSES // X_PIECES
+X_VECTOR_PAIRS = ()
 MU_UNITS = (1, 1, 2, 2, 2, 2, 2, 2, 2)
 LV_UNITS = (2, 2, 2, 2, 2, 2, 2, 1, 1)
 W_BUFS = 6
@@ -162,7 +164,6 @@ def tile_infoncemi_pa_k_kernel(
                 load_queue.remove(load_queue[0])
 
         mu_units = len(MU_UNITS)
-        x_firsts = [sum(X_UNITS[:k]) for k in range(len(X_UNITS))]
 
         if True:
             x_pool = ctx.enter_context(tc.tile_pool(name="x_pool", bufs=X_BUFS))
@@ -173,19 +174,12 @@ def tile_infoncemi_pa_k_kernel(
             w2_raw = {}
             y_rows = prep.tile([P, ROW_TILES, Y_DIM], BF16)
 
-            def load_x(first, passes):
-                chunk = x_pool.tile([P, ROW_TILES, passes * K_PASS], BF16, name="x_chunk", tag="x_chunk")
-                nc.sync.dma_start(
-                    out=chunk[:],
-                    in_=x_samples[:, first * K_PASS : (first + passes) * K_PASS].rearrange(
-                        "(r p) k -> p r k", p=P
-                    ),
-                )
-                words = chunk[:].rearrange("p r k -> p (r k)").bitcast(F32).rearrange(
-                    "n (r g p u) -> n g r u p", r=ROW_TILES, p=P, u=2
-                )
-                for g in range(passes):
-                    x_words[first + g] = words[:, g]
+            def load_x(k):
+                r, piece = divmod(k, X_PIECES)
+                x_rows = x_pool.tile([P, PIECE_PASSES * K_PASS], BF16, name="x_chunk", tag="x_chunk")
+                cols = slice(piece * PIECE_PASSES * K_PASS, (piece + 1) * PIECE_PASSES * K_PASS)
+                nc.sync.dma_start(out=x_rows[:], in_=x_samples[r * P : (r + 1) * P, cols])
+                x_words[k] = x_rows[:].bitcast(F32).rearrange("n (g p u) -> n g u p", p=P, u=2)
 
             def load_w2(head, w2):
                 w2_raw[head] = prep.tile([P, 1, PACK, Y_DIM], BF16, name="w2_raw", tag="w2_raw")
@@ -203,33 +197,31 @@ def tile_infoncemi_pa_k_kernel(
             x_grouped = {}
 
             def x_transpose(k):
-                first, passes = x_firsts[k], X_UNITS[k]
                 x_grouped[k] = xg_pool.tile(
-                    [P, passes * N * PACK], BF16, align_bytes=64, name="x_grouped", tag="x_grouped"
+                    [P, PIECE_PASSES, P * PACK], BF16, align_bytes=64, name="x_grouped", tag="x_grouped"
                 )
-                word_view = x_grouped[k][:].bitcast(F32).rearrange(
-                    "p (g r n u) -> p g r n u", g=passes, r=ROW_TILES, u=2
+                word_view = x_grouped[k][:].rearrange("p g c -> p (g c)").bitcast(F32).rearrange(
+                    "p (g n u) -> p g n u", g=PIECE_PASSES, u=2
                 )
-                for g2 in range(passes):
-                    for half in range(2):
-                        xt_ps = spare_bank([P, 2, 2, P], F32, "xt_ps")
-                        for r2 in range(2):
-                            for u in range(2):
-                                nc.tensor.transpose(
-                                    xt_ps[:, r2, u, :], x_words[first + g2][:, 2 * half + r2, u, :], ident_f32[:]
-                                )
-                        nc.scalar.copy(
-                            out=word_view[:, g2, 2 * half : 2 * half + 2],
-                            in_=xt_ps[:].rearrange("p r u n -> p r n u"),
-                        )
+                for pair in range(PIECE_PASSES // 2):
+                    xt_ps = spare_bank([P, 2, 2, P], F32, "xt_ps")
+                    for g2 in range(2):
+                        for u in range(2):
+                            nc.tensor.transpose(xt_ps[:, g2, u, :], x_words[k][:, 2 * pair + g2, u, :], ident_f32[:])
+                    empty = nc.vector.tensor_copy if pair in X_VECTOR_PAIRS else nc.scalar.copy
+                    empty(
+                        out=word_view[:, 2 * pair : 2 * pair + 2], in_=xt_ps[:].rearrange("p g u n -> p g n u")
+                    )
 
             def x_quantise(k):
-                first, passes = x_firsts[k], X_UNITS[k]
-                nc.vector.quantize_mx(
-                    out=x_codes[:, first : first + passes, :].rearrange("p g n -> p (g n)").bitcast(FP8X4),
-                    scales=x_scales[:, first : first + passes, :].rearrange("p g n -> p (g n)"),
-                    in_=x_grouped[k][:],
-                )
+                r, piece = divmod(k, X_PIECES)
+                for g2 in range(PIECE_PASSES):
+                    g = piece * PIECE_PASSES + g2
+                    nc.vector.quantize_mx(
+                        out=x_codes[:, g, r * P : (r + 1) * P].bitcast(FP8X4),
+                        scales=x_scales[:, g, r * P : (r + 1) * P],
+                        in_=x_grouped[k][:, g2, :],
+                    )
 
             def biases():
                 bias_ps = spare_bank([P, P], BF16, "bias_ps")
@@ -318,12 +310,12 @@ def tile_infoncemi_pa_k_kernel(
                     lambda head=head: w2_quantise(head),
                     (),
                 )
-            for k in range(len(X_UNITS)):
+            for k in range(ROW_TILES * X_PIECES):
                 items["x", k] = (
-                    lambda k=k: load_x(x_firsts[k], X_UNITS[k]),
+                    lambda k=k: load_x(k),
                     lambda k=k: (x_transpose(k), release("x")),
                     lambda k=k: x_quantise(k),
-                    [("x", x_firsts[k] + g) for g in range(X_UNITS[k])],
+                    [("x", k)],
                 )
             for k in range(len(units)):
                 items["w", k] = (
@@ -437,7 +429,7 @@ def tile_infoncemi_pa_k_kernel(
             if previous:
                 previous[0]()
             for head in ("mu", "lv"):
-                while (head, multiplied[head]) in done and ("x", PASSES - 1) in done:
+                while (head, multiplied[head]) in done and ("x", ROW_TILES * X_PIECES - 1) in done:
                     if multiplied[head] == 0:
                         first_bank = PACK * (head == "lv")
                         acc[head] = [bank(first_bank + m, [P, N], F32, "acc") for m in range(PACK)]

@@ -26,7 +26,7 @@ BANKS = 8
 
 FLOPS = 2 * (2 * N * X_DIM * HID + 2 * N * HID * Y_DIM)
 
-RUN = 4
+RUN = 8
 X_PIECES = 2
 PIECE_PASSES = PASSES // X_PIECES
 X_VECTOR_PAIRS = ()

from contextlib import ExitStack

import concourse.mybir as mybir
from concourse.masks import make_identity

F32 = mybir.dt.float32
BF16 = mybir.dt.bfloat16
U32 = mybir.dt.uint32
U8 = mybir.dt.uint8
FP8X4 = mybir.dt.float8_e4m3fn_x4
ACT = mybir.ActivationFunctionType
ALU = mybir.AluOpType

P = 128
PACK = 4
K_PASS = P * PACK

N = 512
X_DIM = 8192
HID = 512
Y_DIM = 512
PASSES = X_DIM // K_PASS
ROW_TILES = N // P
D_TILES = Y_DIM // P
BANKS = 8

FLOPS = 2 * (2 * N * X_DIM * HID + 2 * N * HID * Y_DIM)

RUN = 8
X_PIECES = 2
PIECE_PASSES = PASSES // X_PIECES
X_VECTOR_PAIRS = ()
MU_UNITS = (1, 1, 2, 2, 2, 2, 2, 2, 2)
LV_UNITS = (2, 2, 2, 2, 2, 2, 2, 1, 1)
W_BUFS = 6
X_BUFS = 3
W1_VECTOR_COLUMNS = {"mu": 304, "lv": 240}
W2_VECTOR_COLUMNS = 256
H_VECTOR_COLUMNS = {"mu": 304, "lv": 336}

MU_B1, LV_B1, MU_B2, LV_B2 = 0, 1, 2, 3


def tile_infoncemi_pa_k_kernel(
    tc, x_samples, y_samples, mu_W1, mu_b1, mu_W2, mu_b2, lv_W1, lv_b1, lv_W2, lv_b2, out_0, out_1
):
    nc = tc.nc
    with ExitStack() as ctx:
        const = ctx.enter_context(tc.tile_pool(name="const", bufs=1))
        raw_pool = ctx.enter_context(tc.tile_pool(name="raw_pool", bufs=W_BUFS))
        grouped_pool = ctx.enter_context(tc.tile_pool(name="grouped_pool", bufs=3))
        wq_pool = ctx.enter_context(tc.tile_pool(name="wq_pool", bufs=8))
        psum = ctx.enter_context(tc.psum_pool(name="psum", bufs=1))

        def bank(index, shape, dtype, name):
            return psum.tile(shape, dtype, name=name, tag="bank%d" % (index % BANKS))

        def regroup(dst, src, vector_columns):
            dst_runs = dst.rearrange("p g (c i) t -> p g c t i", i=RUN)
            src_runs = src.rearrange("p g t (c i) -> p g c t i", i=RUN)
            split = vector_columns // RUN
            nc.vector.tensor_copy(out=dst_runs[:, :, :split], in_=src_runs[:, :, :split])
            nc.scalar.copy(out=dst_runs[:, :, split:], in_=src_runs[:, :, split:])

        def quantise(grouped, codes, scales):
            nc.vector.quantize_mx(
                out=codes.bitcast(FP8X4), scales=scales, in_=grouped.rearrange("p g c t -> p (g c t)")
            )

        ident_f32 = const.tile([P, P], F32)
        make_identity(nc, ident_f32[:])
        ident_bf16 = const.tile([P, P], BF16)
        make_identity(nc, ident_bf16[:])
        pos_weight = const.tile([P, P], F32)
        nc.vector.memset(pos_weight[:], -0.5)
        neg_weight = const.tile([P, P], F32)
        nc.vector.memset(neg_weight[:], -0.5 / N)
        ones = const.tile([P, 1], BF16)
        nc.vector.memset(ones[:], 1.0)
        bias_rows = const.tile([P, P], BF16)
        nc.vector.memset(bias_rows[:], 0.0)
        for place, vector in enumerate((mu_b1, lv_b1, mu_b2, lv_b2)):
            nc.scalar.dma_start(
                out=bias_rows[PACK * place : PACK * (place + 1), :], in_=vector.rearrange("(m p) -> m p", p=P)
            )

        x_codes = const.tile([P, PASSES, N], U32, align_bytes=64)
        x_scales = const.tile([P, PASSES, N], U8, align_bytes=64)
        y_t = const.tile([P, D_TILES, N], BF16)
        bias_cols = const.tile([P, 4 * PACK], F32)
        var_y = const.tile([P, D_TILES], F32)
        centre = const.tile([P, D_TILES], F32)
        w2_codes = {}
        w2_scales = {}
        for head in ("mu", "lv"):
            w2_codes[head] = const.tile([P, Y_DIM], U32, align_bytes=64, name="w2_codes_" + head)
            w2_scales[head] = const.tile([P, Y_DIM], U8, align_bytes=64, name="w2_scales_" + head)

        def bias_column(place, m):
            return bias_cols[:, PACK * place + m : PACK * place + m + 1]

        units = []
        for head, w1, sizes in (("mu", mu_W1, MU_UNITS), ("lv", lv_W1, LV_UNITS)):
            first = 0
            for passes in sizes:
                units.append((head, w1, first, passes))
                first += passes
        raw_tiles = {}
        grouped_tiles = {}
        w_quantised = {}

        def load_w(k):
            head, w1, first, passes = units[k]
            raw = raw_pool.tile([P, passes, PACK, HID], BF16, name="raw", tag="raw")
            nc.sync.dma_start(
                out=raw[:],
                in_=w1[first * K_PASS : (first + passes) * K_PASS, :].rearrange(
                    "(g p t) h -> p g t h", p=P, t=PACK
                ),
            )
            raw_tiles[k] = raw

        def w_regroup(k):
            head, w1, first, passes = units[k]
            grouped_tiles[k] = grouped_pool.tile(
                [P, passes, HID, PACK], BF16, align_bytes=64, name="grouped", tag="grouped"
            )
            regroup(grouped_tiles[k][:], raw_tiles[k][:], W1_VECTOR_COLUMNS[head])

        def w_quantise(k):
            head, w1, first, passes = units[k]
            w_codes = wq_pool.tile([P, passes * HID], U32, align_bytes=64, name="w_codes", tag="w_codes")
            w_scales = wq_pool.tile([P, passes * HID], U8, align_bytes=64, name="w_scales", tag="w_scales")
            quantise(grouped_tiles[k][:], w_codes[:], w_scales[:])
            for g2 in range(passes):
                cols = slice(g2 * HID, (g2 + 1) * HID)
                w_quantised[head, first + g2] = (w_codes[:, cols], w_scales[:, cols])

        acc = {}

        def multiply(head, g):
            w_codes, w_scales = w_quantised[head, g]
            for m in range(PACK):
                cols = slice(m * P, (m + 1) * P)
                nc.tensor.matmul_mx(
                    out=acc[head][m][:],
                    lhsT=w_codes[:, cols].bitcast(FP8X4),
                    lhsT_scale=w_scales[:, cols],
                    rhs=x_codes[:, g, :].bitcast(FP8X4),
                    rhs_scale=x_scales[:, g, :],
                    start=(g == 0),
                    stop=(g == PASSES - 1),
                )

        load_queue = []
        buffers_free = {"w": W_BUFS, "x": X_BUFS, "w2": 1}

        def issue_loads():
            while load_queue and buffers_free.get(load_queue[0][0], 1) > 0:
                kind, load = load_queue[0]
                if kind in buffers_free:
                    buffers_free[kind] -= 1
                load()
                load_queue.remove(load_queue[0])

        mu_units = len(MU_UNITS)

        if True:
            x_pool = ctx.enter_context(tc.tile_pool(name="x_pool", bufs=X_BUFS))
            xg_pool = ctx.enter_context(tc.tile_pool(name="xg_pool", bufs=2))
            prep = ctx.enter_context(tc.tile_pool(name="prep", bufs=1))

            x_words = {}
            w2_raw = {}
            y_rows = prep.tile([P, ROW_TILES, Y_DIM], BF16)

            def load_x(k):
                r, piece = divmod(k, X_PIECES)
                x_rows = x_pool.tile([P, PIECE_PASSES * K_PASS], BF16, name="x_chunk", tag="x_chunk")
                cols = slice(piece * PIECE_PASSES * K_PASS, (piece + 1) * PIECE_PASSES * K_PASS)
                nc.sync.dma_start(out=x_rows[:], in_=x_samples[r * P : (r + 1) * P, cols])
                x_words[k] = x_rows[:].bitcast(F32).rearrange("n (g p u) -> n g u p", p=P, u=2)

            def load_w2(head, w2):
                w2_raw[head] = prep.tile([P, 1, PACK, Y_DIM], BF16, name="w2_raw", tag="w2_raw")
                nc.sync.dma_start(out=w2_raw[head][:, 0], in_=w2.rearrange("(t p) d -> p t d", p=P))

            def load_y():
                nc.sync.dma_start(out=y_rows[:], in_=y_samples.rearrange("(r p) d -> p r d", p=P))

            spare_banks = []

            def spare_bank(shape, dtype, name):
                spare_banks.append(name)
                return bank(len(spare_banks), shape, dtype, name)

            x_grouped = {}

            def x_transpose(k):
                x_grouped[k] = xg_pool.tile(
                    [P, PIECE_PASSES, P * PACK], BF16, align_bytes=64, name="x_grouped", tag="x_grouped"
                )
                word_view = x_grouped[k][:].rearrange("p g c -> p (g c)").bitcast(F32).rearrange(
                    "p (g n u) -> p g n u", g=PIECE_PASSES, u=2
                )
                for pair in range(PIECE_PASSES // 2):
                    xt_ps = spare_bank([P, 2, 2, P], F32, "xt_ps")
                    for g2 in range(2):
                        for u in range(2):
                            nc.tensor.transpose(xt_ps[:, g2, u, :], x_words[k][:, 2 * pair + g2, u, :], ident_f32[:])
                    empty = nc.vector.tensor_copy if pair in X_VECTOR_PAIRS else nc.scalar.copy
                    empty(
                        out=word_view[:, 2 * pair : 2 * pair + 2], in_=xt_ps[:].rearrange("p g u n -> p g n u")
                    )

            def x_quantise(k):
                r, piece = divmod(k, X_PIECES)
                for g2 in range(PIECE_PASSES):
                    g = piece * PIECE_PASSES + g2
                    nc.vector.quantize_mx(
                        out=x_codes[:, g, r * P : (r + 1) * P].bitcast(FP8X4),
                        scales=x_scales[:, g, r * P : (r + 1) * P],
                        in_=x_grouped[k][:, g2, :],
                    )

            def biases():
                bias_ps = spare_bank([P, P], BF16, "bias_ps")
                nc.tensor.transpose(bias_ps[:], bias_rows[:], ident_bf16[:])
                nc.vector.tensor_copy(out=bias_cols[:], in_=bias_ps[:, 0 : 4 * PACK])

            sum_y2 = prep.tile([P, D_TILES], F32)
            sums = {}

            def y_sums():
                sums["y"] = spare_bank([P, D_TILES], F32, "sum_ps")
                sums["gram"] = spare_bank([P, D_TILES, P], F32, "gram_ps")
                for j in range(D_TILES):
                    for r in range(ROW_TILES):
                        y_block = y_rows[:, r, j * P : (j + 1) * P]
                        nc.tensor.matmul(
                            out=sums["gram"][:, j, :], lhsT=y_block, rhs=y_block, start=(r == 0), stop=(r == ROW_TILES - 1)
                        )
                    for r in range(ROW_TILES):
                        nc.tensor.matmul(
                            out=sums["y"][:, j : j + 1], lhsT=y_rows[:, r, j * P : (j + 1) * P], rhs=ones[:],
                            start=(r == 0), stop=(r == ROW_TILES - 1),
                        )

            def y_diagonal(j):
                diagonal = prep.tile([P, P], F32, name="diagonal", tag="diagonal")
                nc.vector.scalar_tensor_tensor(
                    out=diagonal[:], in0=sums["gram"][:, j, :], scalar=1.0, in1=ident_f32[:],
                    op0=ALU.mult, op1=ALU.mult, accum_out=sum_y2[:, j : j + 1],
                )

            def y_transpose(j):
                yt_ps = spare_bank([P, N], BF16, "yt_ps")
                for r in range(ROW_TILES):
                    nc.tensor.transpose(
                        yt_ps[:, r * P : (r + 1) * P], y_rows[:, r, j * P : (j + 1) * P], ident_bf16[:]
                    )
                nc.scalar.copy(out=y_t[:, j, :], in_=yt_ps[:])

            def y_moments():
                mean_y = prep.tile([P, D_TILES], F32)
                nc.vector.tensor_scalar(
                    out=mean_y[:], in0=sums["y"][:], scalar1=1.0 / N, scalar2=None, op0=ALU.mult
                )
                mean_sq = prep.tile([P, D_TILES], F32)
                nc.vector.tensor_tensor(out=mean_sq[:], in0=mean_y[:], in1=mean_y[:], op=ALU.mult)
                nc.vector.scalar_tensor_tensor(
                    out=var_y[:], in0=sum_y2[:], scalar=1.0 / N, in1=mean_sq[:],
                    op0=ALU.mult, op1=ALU.subtract,
                )
                nc.vector.tensor_tensor(
                    out=centre[:], in0=bias_cols[:, PACK * MU_B2 : PACK * (MU_B2 + 1)], in1=mean_y[:],
                    op=ALU.subtract,
                )

            w2_grouped = {}

            def w2_regroup(head):
                w2_grouped[head] = prep.tile(
                    [P, 1, Y_DIM, PACK], BF16, align_bytes=64, name="w2_grouped", tag="w2_grouped"
                )
                regroup(w2_grouped[head][:], w2_raw[head][:], W2_VECTOR_COLUMNS)

            def w2_quantise(head):
                quantise(w2_grouped[head][:], w2_codes[head][:], w2_scales[head][:])

            def y_stage_1():
                biases()
                for j in range(D_TILES):
                    y_transpose(j)
                y_sums()

            def y_stage_2():
                for j in range(D_TILES):
                    y_diagonal(j)
                y_moments()

            def release(kind):
                buffers_free[kind] += 1

            items = {"y": (load_y, y_stage_1, y_stage_2, ())}
            for head, w2 in (("mu", mu_W2), ("lv", lv_W2)):
                items["w2", head] = (
                    lambda head=head, w2=w2: load_w2(head, w2),
                    lambda head=head: (w2_regroup(head), release("w2")),
                    lambda head=head: w2_quantise(head),
                    (),
                )
            for k in range(ROW_TILES * X_PIECES):
                items["x", k] = (
                    lambda k=k: load_x(k),
                    lambda k=k: (x_transpose(k), release("x")),
                    lambda k=k: x_quantise(k),
                    [("x", k)],
                )
            for k in range(len(units)):
                items["w", k] = (
                    lambda k=k: load_w(k),
                    lambda k=k: (w_regroup(k), release("w")),
                    lambda k=k: w_quantise(k),
                    [(units[k][0], units[k][2] + g) for g in range(units[k][3])],
                )
        h_pool = ctx.enter_context(tc.tile_pool(name="h_pool", bufs=1))
        term_pool = ctx.enter_context(tc.tile_pool(name="term_pool", bufs=1))
        tail_pool = ctx.enter_context(tc.tile_pool(name="tail_pool", bufs=4))

        h_rows = {}
        h_grouped = {}

        def hidden(head, b1_place, part):
            if head not in h_rows:
                h_rows[head] = h_pool.tile([P, 1, PACK, N], BF16, name="h_rows", tag="h_rows")
            for m in range(PACK):
                if m % 2 == 0:
                    nc.scalar.activation(
                        out=h_rows[head][:, 0, m, part], in_=acc[head][m][:, part], func=ACT.Relu,
                        bias=bias_column(b1_place, m),
                    )
                else:
                    nc.vector.tensor_scalar(
                        out=h_rows[head][:, 0, m, part], in0=acc[head][m][:, part], scalar1=bias_column(b1_place, m),
                        scalar2=0.0, op0=ALU.add, op1=ALU.max,
                    )

        def hidden_regroup(head, part):
            if head not in h_grouped:
                h_grouped[head] = h_pool.tile(
                    [P, 1, N, PACK], BF16, align_bytes=64, name="h_grouped", tag="h_grouped"
                )
            samples = part.stop - part.start
            regroup(
                h_grouped[head][:, :, part, :], h_rows[head][:, :, :, part],
                H_VECTOR_COLUMNS[head] * samples // N // (2 * RUN) * (2 * RUN),
            )

        h_quantised = {}

        def hidden_quantise(head, part):
            if head not in h_quantised:
                h_quantised[head] = (
                    h_pool.tile([P, N], U32, align_bytes=64, name="h_codes", tag="h_codes"),
                    h_pool.tile([P, N], U8, align_bytes=64, name="h_scales", tag="h_scales"),
                )
            h_codes, h_scales = h_quantised[head]
            quantise(h_grouped[head][:, :, part, :], h_codes[:, part], h_scales[:, part])

        second = {}

        def second_layer(head, j, part, bank_index):
            h_codes, h_scales = h_quantised[head]
            product = bank(bank_index, [P, part.stop - part.start], F32, "product")
            nc.tensor.matmul_mx(
                out=product[:],
                lhsT=w2_codes[head][:, j * P : (j + 1) * P].bitcast(FP8X4),
                lhsT_scale=w2_scales[head][:, j * P : (j + 1) * P],
                rhs=h_codes[:, part].bitcast(FP8X4),
                rhs_scale=h_scales[:, part],
                start=True,
                stop=True,
            )
            second[head, j, part.start] = product

        everyone = slice(0, N)
        terms = {}

        def start_terms():
            for sign in ("pos", "neg"):
                terms[sign] = x_pool.tile([P, D_TILES, N], F32, name="terms", tag="x_chunk")

        def mu_terms(j):
            nc.vector.scalar_tensor_tensor(
                out=terms["pos"][:, j, :], in0=second["mu", j, 0][:], scalar=bias_column(MU_B2, j),
                in1=y_t[:, j, :], op0=ALU.add, op1=ALU.subtract,
            )
            nc.scalar.activation(
                out=terms["neg"][:, j, :], in_=second["mu", j, 0][:], func=ACT.Square, bias=centre[:, j : j + 1]
            )

        def pos_square(j):
            nc.scalar.activation(out=terms["pos"][:, j, :], in_=terms["pos"][:, j, :], func=ACT.Square)

        epilogue = (
            (lambda: hidden("mu", MU_B1, everyone), lambda: hidden_regroup("mu", everyone)),
            (
                lambda: hidden_quantise("mu", everyone),
                lambda: [second_layer("mu", j, everyone, j) for j in range(D_TILES)],
            ),
            (lambda: (start_terms(), mu_terms(0)), lambda: (mu_terms(1), pos_square(0))),
            (lambda: pos_square(1), lambda: mu_terms(2)),
            (lambda: (pos_square(2), mu_terms(3)), lambda: pos_square(3)),
        )
        for e in range(len(epilogue)):
            items["mu", e] = (None,) + epilogue[e] + ((),)

        order = (("w", 0), ("w", 1), ("x", 0), ("x", 1), "y", ("w", 2), ("x", 2), ("x", 3), ("w", 3), ("x", 4), ("x", 5), ("w", 4), ("x", 6), ("x", 7), ("w2", "mu"), ("w", 5), ("w", 6), ("w", 7), ("w", 8), ("w2", "lv"), ("w", 9), ("w", 10), ("w", 11), ("w", 12), ("w", 13), ("mu", 0), ("w", 14), ("mu", 1), ("w", 15), ("mu", 2), ("w", 16), ("mu", 3), ("w", 17), ("mu", 4))
        load_queue += [(name[0], items[name][0]) for name in order if items[name][0]]
        issue_loads()
        done = set()
        multiplied = {"mu": 0, "lv": 0}
        previous = None
        for name in order:
            load, stage_1, stage_2, ready = items[name]
            stage_1()
            issue_loads()
            if previous:
                previous[0]()
            for head in ("mu", "lv"):
                while (head, multiplied[head]) in done and ("x", ROW_TILES * X_PIECES - 1) in done:
                    if multiplied[head] == 0:
                        first_bank = PACK * (head == "lv")
                        acc[head] = [bank(first_bank + m, [P, N], F32, "acc") for m in range(PACK)]
                    multiply(head, multiplied[head])
                    multiplied[head] += 1
            if previous:
                done.update(previous[1])
            previous = (stage_2, ready)
        previous[0]()
        for g in range(multiplied["lv"], PASSES):
            multiply("lv", g)

        halves = (slice(0, N // 2), slice(N // 2, N))
        sums_ps = {}

        weight = {}

        def tanh(j, part):
            weight[j, part.start] = tail_pool.tile([P, part.stop - part.start], F32, name="weight", tag="weight")
            nc.scalar.activation(
                out=weight[j, part.start][:], in_=second["lv", j, part.start][:], func=ACT.Tanh, bias=bias_column(LV_B2, j)
            )

        def weight_terms(j, part):
            w = weight[j, part.start]
            nc.scalar.activation(out=w[:], in_=w[:], func=ACT.Exp, scale=-1.0)
            nc.vector.tensor_tensor(
                out=terms["pos"][:, j, part], in0=terms["pos"][:, j, part], in1=w[:], op=ALU.mult
            )
            nc.vector.scalar_tensor_tensor(
                out=terms["neg"][:, j, part], in0=terms["neg"][:, j, part], scalar=var_y[:, j : j + 1], in1=w[:],
                op0=ALU.add, op1=ALU.mult,
            )

        def add_up(j, part, start, stop):
            for i, (sign, weights) in enumerate((("pos", pos_weight), ("neg", neg_weight))):
                nc.tensor.matmul(
                    out=sums_ps[i, part.start][:], lhsT=weights[:], rhs=terms[sign][:, j, part], start=start, stop=stop
                )

        def join(j, part):
            for sign in ("pos", "neg"):
                nc.vector.tensor_tensor(
                    out=terms[sign][:, j, part], in0=terms[sign][:, j, part], in1=terms[sign][:, j - 1, part], op=ALU.add
                )

        for h, part in enumerate(halves):
            hidden("lv", LV_B1, part)
        for h, part in enumerate(halves):
            hidden_regroup("lv", part)
            hidden_quantise("lv", part)
            for j in range(D_TILES):
                second_layer("lv", j, part, PACK * h + j)
        result = term_pool.tile([P, 2, N], F32)
        last = D_TILES - 1
        for h, part in enumerate(halves):
            for i in range(2):
                sums_ps[i, part.start] = bank(2 * h + i, [P, N // 2], F32, "sum_ps")
        pieces = [(j, part) for part in halves for j in range(D_TILES)]

        def store(part):
            nc.scalar.copy(out=result[:, 0, part], in_=sums_ps[0, part.start][:])
            nc.vector.tensor_copy(out=result[:, 1, part], in_=sums_ps[1, part.start][:])
            nc.sync.dma_start(out=out_0.rearrange("(o n) -> o n", o=1)[:, part], in_=result[0:1, 0, part])
            nc.sync.dma_start(out=out_1.rearrange("(o n) -> o n", o=1)[:, part], in_=result[0:1, 1, part])

        tanh(*pieces[0])
        for k, (j, part) in enumerate(pieces):
            if k + 1 < len(pieces):
                tanh(*pieces[k + 1])
            weight_terms(j, part)
            if j < D_TILES - 2:
                add_up(j, part, j == 0, False)
            if j == last:
                join(last, part)
                add_up(last, part, False, True)
            if k == len(pieces) - 1 - 1:
                store(halves[0])
        store(halves[1])
